import numpy as np
import ml_dtypes


def mxq(x, axis, fmt="e4m3"):
    dtype, down = {"e4m3": (ml_dtypes.float8_e4m3fn, 7), "e5m2": (ml_dtypes.float8_e5m2, 14)}[fmt]
    v = np.moveaxis(np.asarray(x, np.float32).astype(ml_dtypes.bfloat16).astype(np.float64), axis, -1)
    blocks = v.reshape(v.shape[:-1] + (-1, 32))
    amax = np.abs(blocks).max(-1, keepdims=True)
    byte = np.maximum(np.where(amax > 0, np.frexp(amax)[1] - 1 + 127, 0) - down, 1)
    scale = np.exp2(byte - 127.0)
    codes = (blocks / scale).astype(np.float32).astype(dtype).astype(np.float64)
    return np.moveaxis((codes * scale).reshape(v.shape), -1, axis)


WIDE = False


def mx_kscale(k):
    if not WIDE:
        return np.ones(k)
    levels = np.array([10, -10, 5, -5, 0])
    a = np.random.permutation(np.resize(levels, k // 512 * 4)).reshape(k // 512, 4)
    idx = np.arange(k)
    return np.exp2(a[idx // 512, idx % 128 // 32])


BF16 = ml_dtypes.bfloat16


def bf(x):
    return np.asarray(x, np.float32).astype(BF16)


def f64(x):
    return np.asarray(x).astype(np.float64)


M, DI, N, DO, TS = 256, 1024, 2048, 1024, 3
DENSITY = 0.25


def setup_inputs():
    k = mx_kscale(N)
    m = (np.random.uniform(size=(N, N)) < DENSITY).astype(np.float64)
    return {'state': bf(np.tanh(1.2 * np.random.standard_normal((M, N))) * k),
            'weights': bf(np.random.standard_normal((N, N)) * 1.5 / np.sqrt(DENSITY * N) / k[:, None]),
            'J': bf(np.random.standard_normal((N, N)) * 2.0 / np.sqrt(DENSITY * N)),
            'theta': bf(np.random.uniform(size=N) * 1.0 + 0.25),
            'lam': bf(0.35 + 0.05 * np.random.standard_normal(1)),
            'mask': bf(m * (1.0 - np.eye(N))),
            'noise_raw': bf(np.random.standard_normal((M, N)) * 2.5),
            'W_out': bf(np.random.standard_normal((DO, N)) * 1.5 / np.sqrt(N)),
            'b_out': bf(np.random.standard_normal(DO) * 0.3)}


def reference(state, weights, J, theta, lam, mask, noise_raw, W_out, b_out):
    st = f64(state)
    eff_w = f64(weights) * f64(mask)
    J_m = f64(J) * f64(mask)
    T = np.abs(np.sin(2.0 * f64(theta)))
    signal = mxq(st, 1, 'e4m3') @ mxq(eff_w, 0, 'e4m3')
    s = np.tanh(st)
    delta = (mxq(s, 1, 'e4m3') @ mxq(J_m, 0, 'e4m3')) * s
    noise = f64(noise_raw) * T * 0.1
    new_state = np.tanh(signal + f64(lam) * delta + noise)
    return (mxq(new_state, 1, 'e4m3') @ mxq(f64(W_out), 1, 'e4m3').T) + f64(b_out)

@@ -1,0 +1,310 @@
+from contextlib import ExitStack
+import math
+
+import concourse.mybir as mybir
+from concourse.masks import make_identity
+
+F32 = mybir.dt.float32
+BF16 = mybir.dt.bfloat16
+U32 = mybir.dt.uint32
+U8 = mybir.dt.uint8
+I32 = mybir.dt.int32
+FP8X4 = mybir.dt.float8_e4m3fn_x4
+ALU = mybir.AluOpType
+ACT = mybir.ActivationFunctionType
+
+P = 128
+ROWS = 256
+NEUR = 2048
+D_OUT = 1024
+G = 512
+NG = NEUR // G
+FLOPS = 2 * ROWS * NEUR * NEUR * 2 + 2 * ROWS * NEUR * D_OUT
+
+CHUNKS = ((0, 2), (2, 1), (3, 1))
+V_EVERY = 8
+V_PHASE = 6
+PI_HI = 3.1415927410125732
+PI_LO = math.pi - PI_HI
+
+
+def tile_brainquantumlayer_pc_kernel(
+    tc, state, weights, J, theta, lam, mask, noise_raw, W_out, b_out, out
+):
+    nc = tc.nc
+    with ExitStack() as ctx:
+        const = ctx.enter_context(tc.tile_pool(name="const", bufs=1))
+        natp = ctx.enter_context(tc.tile_pool(name="natp", bufs=2))
+        mpool = ctx.enter_context(tc.tile_pool(name="mpool", bufs=2))
+        wpool = ctx.enter_context(tc.tile_pool(name="wpool", bufs=3))
+        grp = ctx.enter_context(tc.tile_pool(name="grp", bufs=5))
+        cpool = ctx.enter_context(tc.tile_pool(name="cpool", bufs=5))
+        ep2 = ctx.enter_context(tc.tile_pool(name="ep2", bufs=2))
+        ep1 = ctx.enter_context(tc.tile_pool(name="ep1", bufs=1))
+        acc = ctx.enter_context(tc.psum_pool(name="acc", bufs=2))
+        trp = ctx.enter_context(tc.psum_pool(name="trp", bufs=4))
+
+        w_v = weights.rearrange("(c p j) n -> c p j n", p=P, j=4)
+        j_v = J.rearrange("(c p j) n -> c p j n", p=P, j=4)
+        m_v = mask.rearrange("(c p j) n -> c p j n", p=P, j=4)
+        wo_v = W_out.rearrange("(q t p) n -> q p t n", t=2, p=P)
+
+        steps = [(g0, ng, kp) for (g0, ng) in CHUNKS for kp in range(4)]
+        n_steps = len(steps)
+        raw_m = {}
+        raw_w = {}
+        raw_j = {}
+
+        def load_mask(s):
+            if s < n_steps:
+                g0, ng, kp = steps[s]
+                t = mpool.tile([P, 4, G * ng], BF16, name="m_raw", tag="m_raw")
+                nc.sync.dma_start(out=t[:], in_=m_v[kp, :, :, G * g0 : G * (g0 + ng)])
+                raw_m[s] = t
+
+        def load_wj(s):
+            if s < n_steps:
+                g0, ng, kp = steps[s]
+                t = wpool.tile([P, 4, G * ng], BF16, name="w_raw", tag="w_raw")
+                nc.sync.dma_start(out=t[:], in_=w_v[kp, :, :, G * g0 : G * (g0 + ng)])
+                raw_w[s] = t
+                t = wpool.tile([P, 4, G * ng], BF16, name="j_raw", tag="j_raw")
+                nc.sync.dma_start(out=t[:], in_=j_v[kp, :, :, G * g0 : G * (g0 + ng)])
+                raw_j[s] = t
+
+        th = const.tile([P, NG, 4], BF16, name="th")
+        nc.sync.dma_start(out=th[:], in_=theta.rearrange("(g p i) -> p g i", g=NG, i=4))
+        lam_bf = const.tile([P, 1], BF16, name="lam_bf")
+        nc.sync.dma_start(out=lam_bf[:], in_=lam.partition_broadcast(P))
+        st_nat = natp.tile([P, 2, NEUR], BF16, name="nat", tag="nat")
+        nc.sync.dma_start(out=st_nat[:], in_=state.rearrange("(t p) k -> p t k", p=P))
+        load_mask(0)
+        load_wj(0)
+        nz_nat = natp.tile([P, 2, NEUR], BF16, name="nat", tag="nat")
+        nc.sync.dma_start(out=nz_nat[:], in_=noise_raw.rearrange("(t p) k -> p t k", p=P))
+        brow = grp.tile([P, D_OUT], BF16, name="grp", tag="grp", align_bytes=64)
+        nc.vector.memset(brow[:], 0.0)
+        nc.sync.dma_start(out=brow[0:1, :], in_=b_out.unsqueeze(0))
+        load_mask(1)
+        load_wj(1)
+        load_wj(2)
+
+        ident = const.tile([P, P], F32, name="ident")
+        make_identity(nc, ident[:])
+        ones = const.tile([P, P], BF16, name="ones")
+        nc.vector.memset(ones[:], 1.0)
+        lam_f = const.tile([P, 1], F32, name="lam_f")
+        nc.vector.tensor_copy(out=lam_f[:], in_=lam_bf[:])
+
+        th2 = th[:].rearrange("p g i -> p (g i)")
+        x2 = const.tile([P, 16], F32, name="x2")
+        nc.vector.tensor_scalar(out=x2[:], in0=th2, scalar1=2.0, scalar2=None, op0=ALU.mult)
+        ki = const.tile([P, 16], I32, name="ki")
+        nc.vector.tensor_scalar(out=ki[:], in0=x2[:], scalar1=1.0 / math.pi, scalar2=None, op0=ALU.mult)
+        kf = const.tile([P, 16], F32, name="kf")
+        nc.vector.tensor_copy(out=kf[:], in_=ki[:])
+        r1 = const.tile([P, 16], F32, name="r1")
+        nc.vector.scalar_tensor_tensor(out=r1[:], in0=kf[:], scalar=-PI_HI, in1=x2[:], op0=ALU.mult, op1=ALU.add)
+        r2 = const.tile([P, 16], F32, name="r2")
+        nc.vector.scalar_tensor_tensor(out=r2[:], in0=kf[:], scalar=-PI_LO, in1=r1[:], op0=ALU.mult, op1=ALU.add)
+        sn = const.tile([P, 16], F32, name="sn")
+        nc.scalar.activation(out=sn[:], in_=r2[:], func=ACT.Sin)
+        t01 = const.tile([P, 16], F32, name="t01")
+        nc.scalar.activation(out=t01[:], in_=sn[:], func=ACT.Abs, scale=0.1)
+
+        st_codes = const.tile([P, 4 * ROWS], U32, name="st_codes", align_bytes=64)
+        st_scales = const.tile([P, 4 * ROWS], U8, name="st_scales", align_bytes=64)
+        s_codes = const.tile([P, 4 * ROWS], U32, name="s_codes", align_bytes=64)
+        s_scales = const.tile([P, 4 * ROWS], U8, name="s_scales", align_bytes=64)
+        s_t = const.tile([P, 16, ROWS], F32, name="s_t")
+
+        def word_view(nat_tile):
+            return nat_tile[:].bitcast(F32).rearrange("p t (g c z) -> p t g z c", g=NG, z=2)
+
+        def transposed_bank(words, g):
+            bank = trp.tile([P, 2, 256], F32, name="tr", tag="tr")
+            for z in range(2):
+                for t in range(2):
+                    nc.tensor.transpose(bank[:, z, P * t : P * t + P], words[:, t, g, z, :], ident[:])
+            return bank
+
+        st_words = word_view(st_nat)
+        banks = [transposed_bank(st_words, g) for g in range(NG)]
+        for gp in range(2):
+            half = slice(2 * ROWS * gp, 2 * ROWS * (gp + 1))
+            stg = grp.tile([P, 2048], BF16, name="grp", tag="grp", align_bytes=64)
+            stg_w = stg[:].bitcast(F32).rearrange("p (g m z) -> p g m z", g=2, z=2)
+            for gl in range(2):
+                nc.vector.tensor_copy(out=stg_w[:, gl], in_=banks[2 * gp + gl][:].rearrange("p z m -> p m z"))
+            nc.scalar.activation(
+                out=s_t[:, 8 * gp : 8 * gp + 8, :].rearrange("p (g t) m -> p g t m", g=2),
+                in_=stg[:].rearrange("p (g m t) -> p g t m", g=2, t=4),
+                func=ACT.Tanh,
+            )
+            nc.vector.quantize_mx(out=st_codes[:, half].bitcast(FP8X4), scales=st_scales[:, half], in_=stg[:])
+            sg = grp.tile([P, 2048], BF16, name="grp", tag="grp", align_bytes=64)
+            nc.vector.tensor_copy(
+                out=sg[:].rearrange("p (g m t) -> p g m t", g=2, t=4),
+                in_=s_t[:, 8 * gp : 8 * gp + 8, :].rearrange("p (g t) m -> p g m t", g=2),
+            )
+            nc.vector.quantize_mx(out=s_codes[:, half].bitcast(FP8X4), scales=s_scales[:, half], in_=sg[:])
+
+        bias = const.tile([P, D_OUT], BF16, name="bias")
+        for oc in range(2):
+            pb = trp.tile([P, 512], F32, name="tr", tag="tr")
+            nc.tensor.matmul(out=pb[:], lhsT=ones[:], rhs=brow[:, 512 * oc : 512 * oc + 512], start=True, stop=True)
+            nc.vector.tensor_copy(out=bias[:, 512 * oc : 512 * oc + 512], in_=pb[:])
+
+        noise_t = const.tile([P, 4 * 2 * ROWS * 2], BF16, name="noise_t")
+        noise_w = noise_t[:].bitcast(F32).rearrange("p (g z m) -> p g z m", g=NG, z=2)
+        noise_b = noise_t[:].rearrange("p (g z m e) -> p g z m e", g=NG, z=2, e=2)
+
+        def noise_work():
+            nz_words = word_view(nz_nat)
+            nbanks = [transposed_bank(nz_words, g) for g in range(NG)]
+            for g in range(NG):
+                nc.vector.tensor_copy(out=noise_w[:, g], in_=nbanks[g][:])
+
+        wo_codes = const.tile([P, NG, D_OUT], U32, name="wo_codes", align_bytes=64)
+        wo_scales = const.tile([P, NG, D_OUT], U8, name="wo_scales", align_bytes=64)
+        wo_nat = {}
+
+        def wo_load(q):
+            t = natp.tile([P, 2, NEUR], BF16, name="nat", tag="nat")
+            nc.sync.dma_start(out=t[:], in_=wo_v[q])
+            wo_nat[q] = t
+
+        def wo_work(q):
+            words = word_view(wo_nat[q])
+            wbanks = [transposed_bank(words, g) for g in range(NG)]
+            cols = slice(256 * q, 256 * q + 256)
+            for gp in range(2):
+                gt = grp.tile([P, 2048], BF16, name="grp", tag="grp", align_bytes=64)
+                gw = gt[:].bitcast(F32).rearrange("p (g o z) -> p g o z", g=2, z=2)
+                for gl in range(2):
+                    nc.scalar.copy(out=gw[:, gl], in_=wbanks[2 * gp + gl][:].rearrange("p z o -> p o z"))
+                for gl in range(2):
+                    g = 2 * gp + gl
+                    nc.vector.quantize_mx(
+                        out=wo_codes[:, g, cols].bitcast(FP8X4),
+                        scales=wo_scales[:, g, cols],
+                        in_=gt[:, 1024 * gl : 1024 * gl + 1024],
+                    )
+
+        ns_codes = const.tile([P, NG * ROWS], U32, name="ns_codes", align_bytes=64)
+        ns_scales = const.tile([P, NG * ROWS], U8, name="ns_scales", align_bytes=64)
+        codes = {}
+
+        def multiply(s):
+            nc.vector.tensor_tensor(out=raw_w[s][:], in0=raw_w[s][:], in1=raw_m[s][:], op=ALU.mult)
+            nc.vector.tensor_tensor(out=raw_j[s][:], in0=raw_j[s][:], in1=raw_m[s][:], op=ALU.mult)
+
+        unit_no = [0]
+
+        def regroup_quantise(s):
+            g0, ng, kp = steps[s]
+            for kind, src in ((0, raw_w[s]), (1, raw_j[s])):
+                tagc = "cw" if kind == 0 else "cj"
+                tags = "sw" if kind == 0 else "sj"
+                cd = cpool.tile([P, G * ng], U32, name=tagc, tag=tagc, align_bytes=64)
+                sc = cpool.tile([P, G * ng], U8, name=tags, tag=tags, align_bytes=64)
+                codes[(kind, s)] = (cd, sc)
+                for h in range(ng):
+                    cols = slice(G * h, G * h + G)
+                    gt = grp.tile([P, 2048], BF16, name="grp", tag="grp", align_bytes=64)
+                    dst = gt[:].rearrange("p (i c t) -> p c t i", i=4, t=4)
+                    srcv = src[:, :, cols].rearrange("p t (c i) -> p c t i", i=4)
+                    if unit_no[0] % V_EVERY == V_PHASE:
+                        nc.vector.tensor_copy(out=dst, in_=srcv)
+                    else:
+                        nc.scalar.copy(out=dst, in_=srcv)
+                    unit_no[0] += 1
+                    nc.vector.quantize_mx(out=cd[:, cols].bitcast(FP8X4), scales=sc[:, cols], in_=gt[:])
+
+        def group_work(s_first, h, g):
+            a_t = ep2.tile([P, 4, ROWS], F32, name="a_t", tag="a_t")
+            c_t = ep1.tile([P, 4, ROWS], F32, name="c_t", tag="c_t")
+            for z in range(2):
+                sig = acc.tile([P, 2, ROWS], F32, name="sig", tag="sig")
+                dlt = acc.tile([P, 2, ROWS], F32, name="dlt", tag="dlt")
+                for kind, ps, rc, rs in ((0, sig, st_codes, st_scales), (1, dlt, s_codes, s_scales)):
+                    for e in range(2):
+                        lo = G * h + P * (2 * z + e)
+                        for kp in range(4):
+                            cd, sc = codes[(kind, s_first + kp)]
+                            nc.tensor.matmul_mx(
+                                out=ps[:, e, :],
+                                lhsT=cd[:, lo : lo + P].bitcast(FP8X4),
+                                lhsT_scale=sc[:, lo : lo + P],
+                                rhs=rc[:, ROWS * kp : ROWS * kp + ROWS].bitcast(FP8X4),
+                                rhs_scale=rs[:, ROWS * kp : ROWS * kp + ROWS],
+                                start=(kp == 0),
+                                stop=(kp == 3),
+                            )
+                for e in range(2):
+                    b = 4 * g + 2 * z + e
+                    nc.vector.scalar_tensor_tensor(
+                        out=a_t[:, 2 * z + e, :], in0=noise_b[:, g, z, :, e], scalar=t01[:, b : b + 1],
+                        in1=sig[:, e, :], op0=ALU.mult, op1=ALU.add,
+                    )
+                nc.vector.scalar_tensor_tensor(
+                    out=c_t[:, 2 * z : 2 * z + 2, :], in0=dlt[:], scalar=lam_f[:, 0:1],
+                    in1=s_t[:, 4 * g + 2 * z : 4 * g + 2 * z + 2, :], op0=ALU.mult, op1=ALU.mult,
+                )
+            nc.vector.tensor_tensor(out=a_t[:], in0=a_t[:], in1=c_t[:], op=ALU.add)
+            nsg = ep2.tile([P, ROWS, 4], BF16, name="nsg", tag="nsg", align_bytes=64)
+            nc.scalar.activation(out=nsg[:], in_=a_t[:].rearrange("p t m -> p m t"), func=ACT.Tanh)
+            nc.vector.quantize_mx(
+                out=ns_codes[:, ROWS * g : ROWS * g + ROWS].bitcast(FP8X4),
+                scales=ns_scales[:, ROWS * g : ROWS * g + ROWS],
+                in_=nsg[:].rearrange("p m t -> p (m t)"),
+            )
+
+        ob = {}
+
+        def out_passes(g):
+            for mt in range(2):
+                for oc in range(2):
+                    lo = ROWS * g + P * mt
+                    nc.tensor.matmul_mx(
+                        out=ob[(mt, oc)][:],
+                        lhsT=ns_codes[:, lo : lo + P].bitcast(FP8X4),
+                        lhsT_scale=ns_scales[:, lo : lo + P],
+                        rhs=wo_codes[:, g, 512 * oc : 512 * oc + 512].bitcast(FP8X4),
+                        rhs_scale=wo_scales[:, g, 512 * oc : 512 * oc + 512],
+                        start=(g == 0),
+                        stop=(g == NG - 1),
+                    )
+
+        multiply(0)
+        load_mask(2)
+        for s in range(n_steps):
+            g0, ng, kp = steps[s]
+            if s + 1 < n_steps:
+                multiply(s + 1)
+                load_mask(s + 3)
+            regroup_quantise(s)
+            load_wj(s + 3)
+            if s == 0:
+                noise_work()
+            if 1 <= s <= 4:
+                wo_load(s - 1)
+            if 2 <= s <= 5:
+                wo_work(s - 2)
+            if kp == 3:
+                for h in range(ng):
+                    g = g0 + h
+                    group_work(s - 3, h, g)
+                    if g == NG - 2:
+                        for mt in range(2):
+                            for oc in range(2):
+                                ob[(mt, oc)] = trp.tile([P, 512], F32, name="tr", tag="tr")
+                        for gg in range(NG - 1):
+                            out_passes(gg)
+        out_passes(NG - 1)
+        for mt in range(2):
+            o_sb = ep2.tile([P, D_OUT], F32, name="a_t", tag="a_t")
+            for oc in range(2):
+                cols = slice(512 * oc, 512 * oc + 512)
+                nc.vector.tensor_tensor(out=o_sb[:, cols], in0=ob[(mt, oc)][:], in1=bias[:, cols], op=ALU.add)
+                nc.sync.dma_start(out=out[P * mt : P * mt + P, cols], in_=o_sb[:, cols])

@@ -21,9 +21,12 @@ G = 512
 NG = NEUR // G
 FLOPS = 2 * ROWS * NEUR * NEUR * 2 + 2 * ROWS * NEUR * D_OUT
 
-CHUNKS = ((0, 2), (2, 1), (3, 1))
-V_EVERY = 8
-V_PHASE = 6
+STEPS = (
+    (0, 1, 0), (1, 1, 0), (0, 2, 1), (0, 2, 2), (0, 2, 3),
+    (2, 2, 0), (2, 2, 1), (2, 2, 2), (2, 1, 3), (3, 1, 3),
+)
+PE_EVERY = 4
+PE_MAX = 7
 PI_HI = 3.1415927410125732
 PI_LO = math.pi - PI_HI
 
@@ -35,10 +38,10 @@ def tile_brainquantumlayer_pc_kernel(
     with ExitStack() as ctx:
         const = ctx.enter_context(tc.tile_pool(name="const", bufs=1))
         natp = ctx.enter_context(tc.tile_pool(name="natp", bufs=2))
-        mpool = ctx.enter_context(tc.tile_pool(name="mpool", bufs=2))
+        mpool = ctx.enter_context(tc.tile_pool(name="mpool", bufs=3))
         wpool = ctx.enter_context(tc.tile_pool(name="wpool", bufs=3))
         grp = ctx.enter_context(tc.tile_pool(name="grp", bufs=5))
-        cpool = ctx.enter_context(tc.tile_pool(name="cpool", bufs=5))
+        cpool = ctx.enter_context(tc.tile_pool(name="cpool", bufs=10))
         ep2 = ctx.enter_context(tc.tile_pool(name="ep2", bufs=2))
         ep1 = ctx.enter_context(tc.tile_pool(name="ep1", bufs=1))
         acc = ctx.enter_context(tc.psum_pool(name="acc", bufs=2))
@@ -49,7 +52,7 @@ def tile_brainquantumlayer_pc_kernel(
         m_v = mask.rearrange("(c p j) n -> c p j n", p=P, j=4)
         wo_v = W_out.rearrange("(q t p) n -> q p t n", t=2, p=P)
 
-        steps = [(g0, ng, kp) for (g0, ng) in CHUNKS for kp in range(4)]
+        steps = STEPS
         n_steps = len(steps)
         raw_m = {}
         raw_w = {}
@@ -73,24 +76,26 @@ def tile_brainquantumlayer_pc_kernel(
                 raw_j[s] = t
 
         th = const.tile([P, NG, 4], BF16, name="th")
-        nc.sync.dma_start(out=th[:], in_=theta.rearrange("(g p i) -> p g i", g=NG, i=4))
+        nc.scalar.dma_start(out=th[:], in_=theta.rearrange("(g p i) -> p g i", g=NG, i=4))
         lam_bf = const.tile([P, 1], BF16, name="lam_bf")
-        nc.sync.dma_start(out=lam_bf[:], in_=lam.partition_broadcast(P))
-        st_nat = natp.tile([P, 2, NEUR], BF16, name="nat", tag="nat")
-        nc.sync.dma_start(out=st_nat[:], in_=state.rearrange("(t p) k -> p t k", p=P))
+        nc.scalar.dma_start(out=lam_bf[:], in_=lam.partition_broadcast(P))
         load_mask(0)
         load_wj(0)
-        nz_nat = natp.tile([P, 2, NEUR], BF16, name="nat", tag="nat")
-        nc.sync.dma_start(out=nz_nat[:], in_=noise_raw.rearrange("(t p) k -> p t k", p=P))
+        st_nat = natp.tile([P, 2, NEUR], BF16, name="nat", tag="nat")
+        for t in range(2):
+            nc.sync.dma_start(out=st_nat[:, t, :], in_=state[P * t : P * t + P, :])
+        load_mask(1)
+        load_wj(1)
         brow = grp.tile([P, D_OUT], BF16, name="grp", tag="grp", align_bytes=64)
         nc.vector.memset(brow[:], 0.0)
         nc.sync.dma_start(out=brow[0:1, :], in_=b_out.unsqueeze(0))
-        load_mask(1)
-        load_wj(1)
+        load_mask(2)
         load_wj(2)
 
         ident = const.tile([P, P], F32, name="ident")
         make_identity(nc, ident[:])
+        ident_bf = const.tile([P, P], BF16, name="ident_bf")
+        make_identity(nc, ident_bf[:])
         ones = const.tile([P, P], BF16, name="ones")
         nc.vector.memset(ones[:], 1.0)
         lam_f = const.tile([P, 1], F32, name="lam_f")
@@ -129,19 +134,23 @@ def tile_brainquantumlayer_pc_kernel(
             return bank
 
         st_words = word_view(st_nat)
-        banks = [transposed_bank(st_words, g) for g in range(NG)]
+        stgs = [grp.tile([P, 2048], BF16, name="grp", tag="grp", align_bytes=64) for gp in range(2)]
+        for t in range(2):
+            for gp in range(2):
+                bank = trp.tile([P, 2, 2, P], F32, name="tr", tag="tr")
+                for gl in range(2):
+                    for z in range(2):
+                        nc.tensor.transpose(bank[:, gl, z, :], st_words[:, t, 2 * gp + gl, z, :], ident[:])
+                stg_w = stgs[gp][:].bitcast(F32).rearrange("p (g m z) -> p g m z", g=2, z=2)
+                nc.vector.tensor_copy(out=stg_w[:, :, P * t : P * t + P, :], in_=bank[:].rearrange("p g z m -> p g m z"))
         for gp in range(2):
             half = slice(2 * ROWS * gp, 2 * ROWS * (gp + 1))
-            stg = grp.tile([P, 2048], BF16, name="grp", tag="grp", align_bytes=64)
-            stg_w = stg[:].bitcast(F32).rearrange("p (g m z) -> p g m z", g=2, z=2)
-            for gl in range(2):
-                nc.vector.tensor_copy(out=stg_w[:, gl], in_=banks[2 * gp + gl][:].rearrange("p z m -> p m z"))
             nc.scalar.activation(
                 out=s_t[:, 8 * gp : 8 * gp + 8, :].rearrange("p (g t) m -> p g t m", g=2),
-                in_=stg[:].rearrange("p (g m t) -> p g t m", g=2, t=4),
+                in_=stgs[gp][:].rearrange("p (g m t) -> p g t m", g=2, t=4),
                 func=ACT.Tanh,
             )
-            nc.vector.quantize_mx(out=st_codes[:, half].bitcast(FP8X4), scales=st_scales[:, half], in_=stg[:])
+            nc.vector.quantize_mx(out=st_codes[:, half].bitcast(FP8X4), scales=st_scales[:, half], in_=stgs[gp][:])
             sg = grp.tile([P, 2048], BF16, name="grp", tag="grp", align_bytes=64)
             nc.vector.tensor_copy(
                 out=sg[:].rearrange("p (g m t) -> p g m t", g=2, t=4),
@@ -153,17 +162,22 @@ def tile_brainquantumlayer_pc_kernel(
         for oc in range(2):
             pb = trp.tile([P, 512], F32, name="tr", tag="tr")
             nc.tensor.matmul(out=pb[:], lhsT=ones[:], rhs=brow[:, 512 * oc : 512 * oc + 512], start=True, stop=True)
-            nc.vector.tensor_copy(out=bias[:, 512 * oc : 512 * oc + 512], in_=pb[:])
+            nc.scalar.copy(out=bias[:, 512 * oc : 512 * oc + 512], in_=pb[:])
 
-        noise_t = const.tile([P, 4 * 2 * ROWS * 2], BF16, name="noise_t")
-        noise_w = noise_t[:].bitcast(F32).rearrange("p (g z m) -> p g z m", g=NG, z=2)
-        noise_b = noise_t[:].rearrange("p (g z m e) -> p g z m e", g=NG, z=2, e=2)
+        nz_nat = const.tile([P, 2, NEUR], BF16, name="nz_nat")
 
-        def noise_work():
-            nz_words = word_view(nz_nat)
-            nbanks = [transposed_bank(nz_words, g) for g in range(NG)]
-            for g in range(NG):
-                nc.vector.tensor_copy(out=noise_w[:, g], in_=nbanks[g][:])
+        def noise_load():
+            nc.sync.dma_start(out=nz_nat[:], in_=noise_raw.rearrange("(t p) k -> p t k", p=P))
+
+        noise_3 = const.tile([P, 2, ROWS, 2], BF16, name="noise_3")
+
+        def noise_last():
+            bank = transposed_bank(word_view(nz_nat), NG - 1)
+            nc.scalar.copy(out=noise_3[:].rearrange("p z m e -> p (z m e)").bitcast(F32), in_=bank[:].rearrange("p z m -> p (z m)"))
+
+        def noise_bank(g):
+            bank = transposed_bank(word_view(nz_nat), g)
+            return bank[:].rearrange("p z m -> p (z m)").bitcast(BF16).rearrange("p (z m e) -> p z m e", z=2, e=2)
 
         wo_codes = const.tile([P, NG, D_OUT], U32, name="wo_codes", align_bytes=64)
         wo_scales = const.tile([P, NG, D_OUT], U8, name="wo_scales", align_bytes=64)
@@ -195,116 +209,207 @@ def tile_brainquantumlayer_pc_kernel(
         ns_scales = const.tile([P, NG * ROWS], U8, name="ns_scales", align_bytes=64)
         codes = {}
 
-        def multiply(s):
-            nc.vector.tensor_tensor(out=raw_w[s][:], in0=raw_w[s][:], in1=raw_m[s][:], op=ALU.mult)
-            nc.vector.tensor_tensor(out=raw_j[s][:], in0=raw_j[s][:], in1=raw_m[s][:], op=ALU.mult)
+        def multiply(s, raws):
+            nc.vector.tensor_tensor(out=raws[s][:], in0=raws[s][:], in1=raw_m[s][:], op=ALU.mult)
+
+        def multiply_both(s):
+            multiply(s, raw_w)
+            multiply(s, raw_j)
 
         unit_no = [0]
 
-        def regroup_quantise(s):
-            g0, ng, kp = steps[s]
-            for kind, src in ((0, raw_w[s]), (1, raw_j[s])):
-                tagc = "cw" if kind == 0 else "cj"
-                tags = "sw" if kind == 0 else "sj"
-                cd = cpool.tile([P, G * ng], U32, name=tagc, tag=tagc, align_bytes=64)
-                sc = cpool.tile([P, G * ng], U8, name=tags, tag=tags, align_bytes=64)
-                codes[(kind, s)] = (cd, sc)
-                for h in range(ng):
-                    cols = slice(G * h, G * h + G)
-                    gt = grp.tile([P, 2048], BF16, name="grp", tag="grp", align_bytes=64)
-                    dst = gt[:].rearrange("p (i c t) -> p c t i", i=4, t=4)
-                    srcv = src[:, :, cols].rearrange("p t (c i) -> p c t i", i=4)
-                    if unit_no[0] % V_EVERY == V_PHASE:
-                        nc.vector.tensor_copy(out=dst, in_=srcv)
-                    else:
-                        nc.scalar.copy(out=dst, in_=srcv)
-                    unit_no[0] += 1
-                    nc.vector.quantize_mx(out=cd[:, cols].bitcast(FP8X4), scales=sc[:, cols], in_=gt[:])
+        def regroup(gt, src, z0, z1, on_vector):
+            dst = gt[:].rearrange("p (i c t) -> p c t i", i=4, t=4)[:, :, :, 2 * z0 : 2 * z1]
+            srcv = src.rearrange("p t (c i) -> p c t i", i=4)[:, :, :, 2 * z0 : 2 * z1]
+            if on_vector:
+                nc.vector.tensor_copy(out=dst, in_=srcv)
+            else:
+                nc.scalar.copy(out=dst, in_=srcv)
 
-        def group_work(s_first, h, g):
+        def regroup_on_pe(gt, src):
+            for z in range(2):
+                bank = trp.tile([P, 2, P, 4], BF16, name="tr", tag="tr")
+                for i in range(2):
+                    nc.tensor.matmul(
+                        out=bank[:, i, :, :], lhsT=ident_bf[:],
+                        rhs=src.rearrange("p t (c i) -> p i c t", i=4)[:, 2 * z + i, :, :],
+                        start=True, stop=True,
+                    )
+                nc.scalar.copy(out=gt[:, 1024 * z : 1024 * z + 1024], in_=bank[:].rearrange("p i c t -> p (i c t)"))
+
+        def quantise(gt, cd, sc, z0, z1):
+            cols = slice(256 * z0, 256 * z1)
+            nc.vector.quantize_mx(
+                out=cd[:, cols].bitcast(FP8X4), scales=sc[:, cols], in_=gt[:, 1024 * z0 : 1024 * z1]
+            )
+
+        def unit_tiles(kind, kp, g):
+            tagc = "cw" if kind == 0 else "cj"
+            tags = "sw" if kind == 0 else "sj"
+            cd = cpool.tile([P, G], U32, name=tagc, tag=tagc, align_bytes=64)
+            sc = cpool.tile([P, G], U8, name=tags, tag=tags, align_bytes=64)
+            codes[(kind, kp, g)] = (cd, sc)
+            gt = grp.tile([P, 2048], BF16, name="grp", tag="grp", align_bytes=64)
+            return gt, cd, sc
+
+        def unit(s, kind, h):
+            g0, ng, kp = steps[s]
+            gt, cd, sc = unit_tiles(kind, kp, g0 + h)
+            src = (raw_w if kind == 0 else raw_j)[s][:, :, G * h : G * h + G]
+            n = unit_no[0]
+            unit_no[0] += 1
+            if n % PE_EVERY == PE_EVERY - 1 and n // PE_EVERY < PE_MAX:
+                regroup_on_pe(gt, src)
+            else:
+                regroup(gt, src, 0, 2, False)
+            quantise(gt, cd, sc, 0, 2)
+
+        def block_pass(ps, kind, g, j, kp):
+            rc, rs = (st_codes, st_scales) if kind == 0 else (s_codes, s_scales)
+            cd, sc = codes[(kind, kp, g)]
+            nc.tensor.matmul_mx(
+                out=ps,
+                lhsT=cd[:, P * j : P * j + P].bitcast(FP8X4),
+                lhsT_scale=sc[:, P * j : P * j + P],
+                rhs=rc[:, ROWS * kp : ROWS * kp + ROWS].bitcast(FP8X4),
+                rhs_scale=rs[:, ROWS * kp : ROWS * kp + ROWS],
+                start=(kp == 0),
+                stop=(kp == 3),
+            )
+
+        def big_passes(ps, kind, g, z):
+            for e in range(2):
+                for kp in range(4):
+                    block_pass(ps[:, e, :], kind, g, 2 * z + e, kp)
+
+        def delta_times_s(c_t, dlt, g, z):
+            nc.vector.scalar_tensor_tensor(
+                out=c_t[:, 2 * z : 2 * z + 2, :], in0=dlt[:], scalar=lam_f[:, 0:1],
+                in1=s_t[:, 4 * g + 2 * z : 4 * g + 2 * z + 2, :], op0=ALU.mult, op1=ALU.mult,
+            )
+
+        def tanh_quantise(a_t, nsg, g, m0, m1):
+            nc.scalar.activation(out=nsg[:, m0:m1, :], in_=a_t[:, :, m0:m1].rearrange("p t m -> p m t"), func=ACT.Tanh)
+            nc.vector.quantize_mx(
+                out=ns_codes[:, ROWS * g + m0 : ROWS * g + m1].bitcast(FP8X4),
+                scales=ns_scales[:, ROWS * g + m0 : ROWS * g + m1],
+                in_=nsg[:, m0:m1, :].rearrange("p m t -> p (m t)"),
+            )
+
+        def group_work(g):
             a_t = ep2.tile([P, 4, ROWS], F32, name="a_t", tag="a_t")
             c_t = ep1.tile([P, 4, ROWS], F32, name="c_t", tag="c_t")
+            noise_b = noise_bank(g)
+            sigs = []
             for z in range(2):
                 sig = acc.tile([P, 2, ROWS], F32, name="sig", tag="sig")
                 dlt = acc.tile([P, 2, ROWS], F32, name="dlt", tag="dlt")
-                for kind, ps, rc, rs in ((0, sig, st_codes, st_scales), (1, dlt, s_codes, s_scales)):
-                    for e in range(2):
-                        lo = G * h + P * (2 * z + e)
-                        for kp in range(4):
-                            cd, sc = codes[(kind, s_first + kp)]
-                            nc.tensor.matmul_mx(
-                                out=ps[:, e, :],
-                                lhsT=cd[:, lo : lo + P].bitcast(FP8X4),
-                                lhsT_scale=sc[:, lo : lo + P],
-                                rhs=rc[:, ROWS * kp : ROWS * kp + ROWS].bitcast(FP8X4),
-                                rhs_scale=rs[:, ROWS * kp : ROWS * kp + ROWS],
-                                start=(kp == 0),
-                                stop=(kp == 3),
-                            )
-                for e in range(2):
-                    b = 4 * g + 2 * z + e
-                    nc.vector.scalar_tensor_tensor(
-                        out=a_t[:, 2 * z + e, :], in0=noise_b[:, g, z, :, e], scalar=t01[:, b : b + 1],
-                        in1=sig[:, e, :], op0=ALU.mult, op1=ALU.add,
-                    )
+                sigs.append(sig)
+                big_passes(sig, 0, g, z)
+                big_passes(dlt, 1, g, z)
+                delta_times_s(c_t, dlt, g, z)
+            for j in range(4):
                 nc.vector.scalar_tensor_tensor(
-                    out=c_t[:, 2 * z : 2 * z + 2, :], in0=dlt[:], scalar=lam_f[:, 0:1],
-                    in1=s_t[:, 4 * g + 2 * z : 4 * g + 2 * z + 2, :], op0=ALU.mult, op1=ALU.mult,
+                    out=c_t[:, j, :], in0=noise_b[:, j // 2, :, j % 2], scalar=t01[:, 4 * g + j : 4 * g + j + 1],
+                    in1=c_t[:, j, :], op0=ALU.mult, op1=ALU.add,
                 )
-            nc.vector.tensor_tensor(out=a_t[:], in0=a_t[:], in1=c_t[:], op=ALU.add)
+            for z in range(2):
+                nc.vector.tensor_tensor(
+                    out=a_t[:, 2 * z : 2 * z + 2, :], in0=sigs[z][:], in1=c_t[:, 2 * z : 2 * z + 2, :], op=ALU.add
+                )
             nsg = ep2.tile([P, ROWS, 4], BF16, name="nsg", tag="nsg", align_bytes=64)
-            nc.scalar.activation(out=nsg[:], in_=a_t[:].rearrange("p t m -> p m t"), func=ACT.Tanh)
-            nc.vector.quantize_mx(
-                out=ns_codes[:, ROWS * g : ROWS * g + ROWS].bitcast(FP8X4),
-                scales=ns_scales[:, ROWS * g : ROWS * g + ROWS],
-                in_=nsg[:].rearrange("p m t -> p (m t)"),
-            )
+            tanh_quantise(a_t, nsg, g, 0, ROWS)
 
         ob = {}
 
-        def out_passes(g):
-            for mt in range(2):
-                for oc in range(2):
-                    lo = ROWS * g + P * mt
-                    nc.tensor.matmul_mx(
-                        out=ob[(mt, oc)][:],
-                        lhsT=ns_codes[:, lo : lo + P].bitcast(FP8X4),
-                        lhsT_scale=ns_scales[:, lo : lo + P],
-                        rhs=wo_codes[:, g, 512 * oc : 512 * oc + 512].bitcast(FP8X4),
-                        rhs_scale=wo_scales[:, g, 512 * oc : 512 * oc + 512],
-                        start=(g == 0),
-                        stop=(g == NG - 1),
-                    )
+        def out_pass(g, mt, oc):
+            lo = ROWS * g + P * mt
+            nc.tensor.matmul_mx(
+                out=ob[(mt, oc)][:],
+                lhsT=ns_codes[:, lo : lo + P].bitcast(FP8X4),
+                lhsT_scale=ns_scales[:, lo : lo + P],
+                rhs=wo_codes[:, g, 512 * oc : 512 * oc + 512].bitcast(FP8X4),
+                rhs_scale=wo_scales[:, g, 512 * oc : 512 * oc + 512],
+                start=(g == 0),
+                stop=(g == NG - 1),
+            )
 
-        multiply(0)
-        load_mask(2)
+        def last_step(s):
+            g = NG - 1
+            a_t = ep2.tile([P, 4, ROWS], F32, name="a_t", tag="a_t")
+            c_t = ep1.tile([P, 4, ROWS], F32, name="c_t", tag="c_t")
+            unit(s, 0, 0)
+            gt, cd, sc = unit_tiles(1, 3, g)
+            for z in (1, 0):
+                regroup(gt, raw_j[s][:, :, 0:G], z, z + 1, z == 1)
+            for z in (1, 0):
+                sig = acc.tile([P, 2, ROWS], F32, name="sig", tag="sig")
+                big_passes(sig, 0, g, z)
+                for e in range(2):
+                    j = 2 * z + e
+                    nc.vector.scalar_tensor_tensor(
+                        out=a_t[:, j, :], in0=noise_3[:, z, :, e], scalar=t01[:, 4 * g + j : 4 * g + j + 1],
+                        in1=sig[:, e, :], op0=ALU.mult, op1=ALU.add,
+                    )
+            dlts = {}
+            for j in (2, 3, 0, 1):
+                tag = "dlt" if j >= 2 else "sig"
+                dlts[j] = acc.tile([P, 2, ROWS], F32, name=tag, tag=tag)
+                for kp in range(3):
+                    block_pass(dlts[j][:, 0, :], 1, g, j, kp)
+            for z in (1, 0):
+                quantise(gt, cd, sc, z, z + 1)
+                for j in (2 * z, 2 * z + 1):
+                    block_pass(dlts[j][:, 0, :], 1, g, j, 3)
+            for z in (1, 0):
+                for j in (2 * z, 2 * z + 1):
+                    nc.vector.scalar_tensor_tensor(
+                        out=c_t[:, j, :], in0=dlts[j][:, 0, :], scalar=lam_f[:, 0:1],
+                        in1=s_t[:, 4 * g + j, :], op0=ALU.mult, op1=ALU.mult,
+                    )
+                zz = slice(2 * z, 2 * z + 2)
+                nc.vector.tensor_tensor(out=a_t[:, zz, :], in0=a_t[:, zz, :], in1=c_t[:, zz, :], op=ALU.add)
+            nsg = ep2.tile([P, ROWS, 4], BF16, name="nsg", tag="nsg", align_bytes=64)
+            for mt in range(2):
+                tanh_quantise(a_t, nsg, g, P * mt, P * mt + P)
+                o_sb = ep2.tile([P, D_OUT], F32, name="a_t", tag="a_t")
+                for oc in range(2):
+                    out_pass(g, mt, oc)
+                    cols = slice(512 * oc, 512 * oc + 512)
+                    nc.vector.tensor_tensor(out=o_sb[:, cols], in0=ob[(mt, oc)][:], in1=bias[:, cols], op=ALU.add)
+                    nc.sync.dma_start(out=out[P * mt : P * mt + P, cols], in_=o_sb[:, cols])
+
+        WO_LOAD = {1: 0, 2: 1, 4: 2, 5: 3}
+        WO_WORK = {4: 0, 5: 1, 7: 2, 8: 3}
+        multiply_both(0)
         for s in range(n_steps):
             g0, ng, kp = steps[s]
             if s + 1 < n_steps:
-                multiply(s + 1)
-                load_mask(s + 3)
-            regroup_quantise(s)
+                multiply_both(s + 1)
+            if s == n_steps - 1:
+                last_step(s)
+                break
+            for kind in range(2):
+                for h in range(ng):
+                    unit(s, kind, h)
+            load_mask(s + 3)
             load_wj(s + 3)
             if s == 0:
-                noise_work()
-            if 1 <= s <= 4:
-                wo_load(s - 1)
-            if 2 <= s <= 5:
-                wo_work(s - 2)
+                noise_load()
+            if s in WO_LOAD:
+                wo_load(WO_LOAD[s])
+            if s in WO_WORK:
+                wo_work(WO_WORK[s])
+            if s == 7:
+                noise_last()
             if kp == 3:
-                for h in range(ng):
-                    g = g0 + h
-                    group_work(s - 3, h, g)
-                    if g == NG - 2:
+                for g in range(g0, g0 + ng):
+                    group_work(g)
+                if g0 + ng == NG - 1:
+                    for mt in range(2):
+                        for oc in range(2):
+                            ob[(mt, oc)] = trp.tile([P, 512], F32, name="tr", tag="tr")
+                    for gg in range(NG - 1):
                         for mt in range(2):
                             for oc in range(2):
-                                ob[(mt, oc)] = trp.tile([P, 512], F32, name="tr", tag="tr")
-                        for gg in range(NG - 1):
-                            out_passes(gg)
-        out_passes(NG - 1)
-        for mt in range(2):
-            o_sb = ep2.tile([P, D_OUT], F32, name="a_t", tag="a_t")
-            for oc in range(2):
-                cols = slice(512 * oc, 512 * oc + 512)
-                nc.vector.tensor_tensor(out=o_sb[:, cols], in0=ob[(mt, oc)][:], in1=bias[:, cols], op=ALU.add)
-                nc.sync.dma_start(out=out[P * mt : P * mt + P, cols], in_=o_sb[:, cols])
+                                out_pass(gg, mt, oc)

@@ -22,11 +22,15 @@ NG = NEUR // G
 FLOPS = 2 * ROWS * NEUR * NEUR * 2 + 2 * ROWS * NEUR * D_OUT
 
 STEPS = (
-    (0, 1, 0), (1, 1, 0), (0, 2, 1), (0, 2, 2), (0, 2, 3),
-    (2, 2, 0), (2, 2, 1), (2, 2, 2), (2, 1, 3), (3, 1, 3),
+    (0, 1, 0), (1, 1, 0), (0, 1, 1), (1, 1, 1), (0, 2, 2), (0, 2, 3),
+    (2, 2, 0), (2, 2, 1), (2, 1, 2), (2, 1, 3), (3, 1, 2), (3, 1, 3),
 )
 PE_EVERY = 4
 PE_MAX = 7
+V_EVERY = 16
+V_PHASE = 9
+MULT_LEAD = 2
+QUANT_LAG = 2
 PI_HI = 3.1415927410125732
 PI_LO = math.pi - PI_HI
 
@@ -46,51 +50,59 @@ def tile_brainquantumlayer_pc_kernel(
         ep1 = ctx.enter_context(tc.tile_pool(name="ep1", bufs=1))
         acc = ctx.enter_context(tc.psum_pool(name="acc", bufs=2))
         trp = ctx.enter_context(tc.psum_pool(name="trp", bufs=4))
+        ctx.enter_context(tc.manual_schedule())
 
         w_v = weights.rearrange("(c p j) n -> c p j n", p=P, j=4)
         j_v = J.rearrange("(c p j) n -> c p j n", p=P, j=4)
         m_v = mask.rearrange("(c p j) n -> c p j n", p=P, j=4)
         wo_v = W_out.rearrange("(q t p) n -> q p t n", t=2, p=P)
 
-        steps = STEPS
-        n_steps = len(steps)
+        units = []
+        unit_step = []
+        for s, (g0, ng, kp) in enumerate(STEPS):
+            by_group = [(kind, kp, g0 + h) for h in range(ng) for kind in range(2)]
+            by_kind = [(kind, kp, g0 + h) for kind in range(2) for h in range(ng)]
+            order = by_group if kp == 3 else by_kind
+            units.extend(order)
+            unit_step.extend([s] * len(order))
+        n_units = len(units)
         raw_m = {}
-        raw_w = {}
-        raw_j = {}
+        raw = {}
 
-        def load_mask(s):
-            if s < n_steps:
-                g0, ng, kp = steps[s]
+        def load_step(s):
+            if s < len(STEPS):
+                g0, ng, kp = STEPS[s]
+                cols = slice(G * g0, G * (g0 + ng))
                 t = mpool.tile([P, 4, G * ng], BF16, name="m_raw", tag="m_raw")
-                nc.sync.dma_start(out=t[:], in_=m_v[kp, :, :, G * g0 : G * (g0 + ng)])
+                nc.sync.dma_start(out=t[:], in_=m_v[kp, :, :, cols])
                 raw_m[s] = t
+                for kind, view in ((0, w_v), (1, j_v)):
+                    name = "w_raw" if kind == 0 else "j_raw"
+                    t = wpool.tile([P, 4, G * ng], BF16, name=name, tag=name)
+                    nc.sync.dma_start(out=t[:], in_=view[kp, :, :, cols])
+                    raw[(kind, s)] = t
 
-        def load_wj(s):
-            if s < n_steps:
-                g0, ng, kp = steps[s]
-                t = wpool.tile([P, 4, G * ng], BF16, name="w_raw", tag="w_raw")
-                nc.sync.dma_start(out=t[:], in_=w_v[kp, :, :, G * g0 : G * (g0 + ng)])
-                raw_w[s] = t
-                t = wpool.tile([P, 4, G * ng], BF16, name="j_raw", tag="j_raw")
-                nc.sync.dma_start(out=t[:], in_=j_v[kp, :, :, G * g0 : G * (g0 + ng)])
-                raw_j[s] = t
+        wo_nat = {}
+
+        def wo_load(q):
+            t = natp.tile([P, 2, NEUR], BF16, name="nat", tag="nat")
+            nc.sync.dma_start(out=t[:], in_=wo_v[q])
+            wo_nat[q] = t
 
         th = const.tile([P, NG, 4], BF16, name="th")
         nc.scalar.dma_start(out=th[:], in_=theta.rearrange("(g p i) -> p g i", g=NG, i=4))
         lam_bf = const.tile([P, 1], BF16, name="lam_bf")
         nc.scalar.dma_start(out=lam_bf[:], in_=lam.partition_broadcast(P))
-        load_mask(0)
-        load_wj(0)
+        brow = grp.tile([P, D_OUT], BF16, name="grp", tag="grp", align_bytes=64)
+        nc.gpsimd.memset(brow[:], 0.0)
+        nc.scalar.dma_start(out=brow[0:1, :], in_=b_out.unsqueeze(0))
+        load_step(0)
+        load_step(1)
         st_nat = natp.tile([P, 2, NEUR], BF16, name="nat", tag="nat")
         for t in range(2):
             nc.sync.dma_start(out=st_nat[:, t, :], in_=state[P * t : P * t + P, :])
-        load_mask(1)
-        load_wj(1)
-        brow = grp.tile([P, D_OUT], BF16, name="grp", tag="grp", align_bytes=64)
-        nc.vector.memset(brow[:], 0.0)
-        nc.sync.dma_start(out=brow[0:1, :], in_=b_out.unsqueeze(0))
-        load_mask(2)
-        load_wj(2)
+        load_step(2)
+        nz_nat = const.tile([P, 2, NEUR], BF16, name="nz_nat")
 
         ident = const.tile([P, P], F32, name="ident")
         make_identity(nc, ident[:])
@@ -117,6 +129,12 @@ def tile_brainquantumlayer_pc_kernel(
         t01 = const.tile([P, 16], F32, name="t01")
         nc.scalar.activation(out=t01[:], in_=sn[:], func=ACT.Abs, scale=0.1)
 
+        bias = const.tile([P, D_OUT], BF16, name="bias")
+        for oc in range(2):
+            pb = trp.tile([P, 512], F32, name="tr", tag="tr")
+            nc.tensor.matmul(out=pb[:], lhsT=ones[:], rhs=brow[:, 512 * oc : 512 * oc + 512], start=True, stop=True)
+            nc.scalar.copy(out=bias[:, 512 * oc : 512 * oc + 512], in_=pb[:])
+
         st_codes = const.tile([P, 4 * ROWS], U32, name="st_codes", align_bytes=64)
         st_scales = const.tile([P, 4 * ROWS], U8, name="st_scales", align_bytes=64)
         s_codes = const.tile([P, 4 * ROWS], U32, name="s_codes", align_bytes=64)
@@ -133,43 +151,46 @@ def tile_brainquantumlayer_pc_kernel(
                     nc.tensor.transpose(bank[:, z, P * t : P * t + P], words[:, t, g, z, :], ident[:])
             return bank
 
-        st_words = word_view(st_nat)
-        stgs = [grp.tile([P, 2048], BF16, name="grp", tag="grp", align_bytes=64) for gp in range(2)]
-        for t in range(2):
-            for gp in range(2):
-                bank = trp.tile([P, 2, 2, P], F32, name="tr", tag="tr")
-                for gl in range(2):
-                    for z in range(2):
-                        nc.tensor.transpose(bank[:, gl, z, :], st_words[:, t, 2 * gp + gl, z, :], ident[:])
-                stg_w = stgs[gp][:].bitcast(F32).rearrange("p (g m z) -> p g m z", g=2, z=2)
-                nc.vector.tensor_copy(out=stg_w[:, :, P * t : P * t + P, :], in_=bank[:].rearrange("p g z m -> p g m z"))
-        for gp in range(2):
-            half = slice(2 * ROWS * gp, 2 * ROWS * (gp + 1))
+        stgs = {}
+        sgs = {}
+
+        def state_gather(gp):
+            words = word_view(st_nat)
+            stg = grp.tile([P, 2048], BF16, name="grp", tag="grp", align_bytes=64)
+            stg_w = stg[:].bitcast(F32).rearrange("p (g m z) -> p g m z", g=2, z=2)
+            for gl in range(2):
+                bank = transposed_bank(words, 2 * gp + gl)
+                nc.vector.tensor_copy(out=stg_w[:, gl], in_=bank[:].rearrange("p z m -> p m z"))
+            stgs[gp] = stg
+
+        def state_half(gp):
+            return slice(2 * ROWS * gp, 2 * ROWS * (gp + 1))
+
+        def state_tanh(gp):
             nc.scalar.activation(
                 out=s_t[:, 8 * gp : 8 * gp + 8, :].rearrange("p (g t) m -> p g t m", g=2),
                 in_=stgs[gp][:].rearrange("p (g m t) -> p g t m", g=2, t=4),
                 func=ACT.Tanh,
             )
+            half = state_half(gp)
             nc.vector.quantize_mx(out=st_codes[:, half].bitcast(FP8X4), scales=st_scales[:, half], in_=stgs[gp][:])
+
+        def state_round(gp):
             sg = grp.tile([P, 2048], BF16, name="grp", tag="grp", align_bytes=64)
             nc.vector.tensor_copy(
                 out=sg[:].rearrange("p (g m t) -> p g m t", g=2, t=4),
                 in_=s_t[:, 8 * gp : 8 * gp + 8, :].rearrange("p (g t) m -> p g m t", g=2),
             )
-            nc.vector.quantize_mx(out=s_codes[:, half].bitcast(FP8X4), scales=s_scales[:, half], in_=sg[:])
+            sgs[gp] = sg
 
-        bias = const.tile([P, D_OUT], BF16, name="bias")
-        for oc in range(2):
-            pb = trp.tile([P, 512], F32, name="tr", tag="tr")
-            nc.tensor.matmul(out=pb[:], lhsT=ones[:], rhs=brow[:, 512 * oc : 512 * oc + 512], start=True, stop=True)
-            nc.scalar.copy(out=bias[:, 512 * oc : 512 * oc + 512], in_=pb[:])
+        def state_quantise(gp):
+            half = state_half(gp)
+            nc.vector.quantize_mx(out=s_codes[:, half].bitcast(FP8X4), scales=s_scales[:, half], in_=sgs[gp][:])
 
-        nz_nat = const.tile([P, 2, NEUR], BF16, name="nz_nat")
+        noise_3 = const.tile([P, 2, ROWS, 2], BF16, name="noise_3")
 
         def noise_load():
             nc.sync.dma_start(out=nz_nat[:], in_=noise_raw.rearrange("(t p) k -> p t k", p=P))
-
-        noise_3 = const.tile([P, 2, ROWS, 2], BF16, name="noise_3")
 
         def noise_last():
             bank = transposed_bank(word_view(nz_nat), NG - 1)
@@ -181,44 +202,45 @@ def tile_brainquantumlayer_pc_kernel(
 
         wo_codes = const.tile([P, NG, D_OUT], U32, name="wo_codes", align_bytes=64)
         wo_scales = const.tile([P, NG, D_OUT], U8, name="wo_scales", align_bytes=64)
-        wo_nat = {}
+        wo_gt = {}
 
-        def wo_load(q):
-            t = natp.tile([P, 2, NEUR], BF16, name="nat", tag="nat")
-            nc.sync.dma_start(out=t[:], in_=wo_v[q])
-            wo_nat[q] = t
+        def wo_gather(q, gp):
+            gt = grp.tile([P, 2048], BF16, name="grp", tag="grp", align_bytes=64)
+            gw = gt[:].bitcast(F32).rearrange("p (g o z) -> p g o z", g=2, z=2)
+            for gl in range(2):
+                bank = transposed_bank(word_view(wo_nat[q]), 2 * gp + gl)
+                nc.scalar.copy(out=gw[:, gl], in_=bank[:].rearrange("p z o -> p o z"))
+            wo_gt[(q, gp)] = gt
 
-        def wo_work(q):
-            words = word_view(wo_nat[q])
-            wbanks = [transposed_bank(words, g) for g in range(NG)]
+        def wo_quantise(q, gp):
             cols = slice(256 * q, 256 * q + 256)
-            for gp in range(2):
-                gt = grp.tile([P, 2048], BF16, name="grp", tag="grp", align_bytes=64)
-                gw = gt[:].bitcast(F32).rearrange("p (g o z) -> p g o z", g=2, z=2)
-                for gl in range(2):
-                    nc.scalar.copy(out=gw[:, gl], in_=wbanks[2 * gp + gl][:].rearrange("p z o -> p o z"))
-                for gl in range(2):
-                    g = 2 * gp + gl
-                    nc.vector.quantize_mx(
-                        out=wo_codes[:, g, cols].bitcast(FP8X4),
-                        scales=wo_scales[:, g, cols],
-                        in_=gt[:, 1024 * gl : 1024 * gl + 1024],
-                    )
+            for gl in range(2):
+                nc.vector.quantize_mx(
+                    out=wo_codes[:, 2 * gp + gl, cols].bitcast(FP8X4),
+                    scales=wo_scales[:, 2 * gp + gl, cols],
+                    in_=wo_gt[(q, gp)][:, 1024 * gl : 1024 * gl + 1024],
+                )
 
         ns_codes = const.tile([P, NG * ROWS], U32, name="ns_codes", align_bytes=64)
         ns_scales = const.tile([P, NG * ROWS], U8, name="ns_scales", align_bytes=64)
         codes = {}
+        gts = {}
+        multiplied = set()
 
-        def multiply(s, raws):
-            nc.vector.tensor_tensor(out=raws[s][:], in0=raws[s][:], in1=raw_m[s][:], op=ALU.mult)
+        def multiply_for(u):
+            if u < n_units:
+                key = (units[u][0], unit_step[u])
+                if key not in multiplied:
+                    multiplied.add(key)
+                    t = raw[key]
+                    nc.vector.tensor_tensor(out=t[:], in0=t[:], in1=raw_m[key[1]][:], op=ALU.mult)
 
-        def multiply_both(s):
-            multiply(s, raw_w)
-            multiply(s, raw_j)
+        def source(u):
+            kind, kp, g = units[u]
+            h = g - STEPS[unit_step[u]][0]
+            return raw[(kind, unit_step[u])][:, :, G * h : G * h + G]
 
-        unit_no = [0]
-
-        def regroup(gt, src, z0, z1, on_vector):
+        def regroup_part(gt, src, z0, z1, on_vector):
             dst = gt[:].rearrange("p (i c t) -> p c t i", i=4, t=4)[:, :, :, 2 * z0 : 2 * z1]
             srcv = src.rearrange("p t (c i) -> p c t i", i=4)[:, :, :, 2 * z0 : 2 * z1]
             if on_vector:
@@ -226,43 +248,55 @@ def tile_brainquantumlayer_pc_kernel(
             else:
                 nc.scalar.copy(out=dst, in_=srcv)
 
-        def regroup_on_pe(gt, src):
+        pe_banks = {}
+
+        def on_pe(u):
+            return u % PE_EVERY == PE_EVERY - 1 and u // PE_EVERY < PE_MAX
+
+        def interleave_on_pe(u):
+            src = source(u)
             for z in range(2):
                 bank = trp.tile([P, 2, P, 4], BF16, name="tr", tag="tr")
+                pe_banks[(u, z)] = bank
                 for i in range(2):
                     nc.tensor.matmul(
                         out=bank[:, i, :, :], lhsT=ident_bf[:],
                         rhs=src.rearrange("p t (c i) -> p i c t", i=4)[:, 2 * z + i, :, :],
                         start=True, stop=True,
                     )
-                nc.scalar.copy(out=gt[:, 1024 * z : 1024 * z + 1024], in_=bank[:].rearrange("p i c t -> p (i c t)"))
 
-        def quantise(gt, cd, sc, z0, z1):
-            cols = slice(256 * z0, 256 * z1)
-            nc.vector.quantize_mx(
-                out=cd[:, cols].bitcast(FP8X4), scales=sc[:, cols], in_=gt[:, 1024 * z0 : 1024 * z1]
-            )
+        def regroup(u):
+            gt = grp.tile([P, 2048], BF16, name="grp", tag="grp", align_bytes=64)
+            gts[u] = gt
+            if on_pe(u):
+                for z in range(2):
+                    half = slice(1024 * z, 1024 * z + 1024)
+                    nc.scalar.copy(out=gt[:, half], in_=pe_banks[(u, z)][:].rearrange("p i c t -> p (i c t)"))
+            elif u == n_units - 1:
+                for z in (1, 0):
+                    regroup_part(gt, source(u), z, z + 1, z == 1)
+            else:
+                regroup_part(gt, source(u), 0, 2, u % V_EVERY == V_PHASE)
 
-        def unit_tiles(kind, kp, g):
+        def code_tiles(u):
+            kind = units[u][0]
             tagc = "cw" if kind == 0 else "cj"
             tags = "sw" if kind == 0 else "sj"
             cd = cpool.tile([P, G], U32, name=tagc, tag=tagc, align_bytes=64)
             sc = cpool.tile([P, G], U8, name=tags, tag=tags, align_bytes=64)
-            codes[(kind, kp, g)] = (cd, sc)
-            gt = grp.tile([P, 2048], BF16, name="grp", tag="grp", align_bytes=64)
-            return gt, cd, sc
+            codes[units[u]] = (cd, sc)
 
-        def unit(s, kind, h):
-            g0, ng, kp = steps[s]
-            gt, cd, sc = unit_tiles(kind, kp, g0 + h)
-            src = (raw_w if kind == 0 else raw_j)[s][:, :, G * h : G * h + G]
-            n = unit_no[0]
-            unit_no[0] += 1
-            if n % PE_EVERY == PE_EVERY - 1 and n // PE_EVERY < PE_MAX:
-                regroup_on_pe(gt, src)
-            else:
-                regroup(gt, src, 0, 2, False)
-            quantise(gt, cd, sc, 0, 2)
+        def quantise_part(u, z0, z1):
+            cd, sc = codes[units[u]]
+            cols = slice(256 * z0, 256 * z1)
+            nc.vector.quantize_mx(
+                out=cd[:, cols].bitcast(FP8X4), scales=sc[:, cols], in_=gts[u][:, 1024 * z0 : 1024 * z1]
+            )
+
+        def quantise(u):
+            if 0 <= u < n_units:
+                code_tiles(u)
+                quantise_part(u, 0, 2)
 
         def block_pass(ps, kind, g, j, kp):
             rc, rs = (st_codes, st_scales) if kind == 0 else (s_codes, s_scales)
@@ -282,43 +316,76 @@ def tile_brainquantumlayer_pc_kernel(
                 for kp in range(4):
                     block_pass(ps[:, e, :], kind, g, 2 * z + e, kp)
 
-        def delta_times_s(c_t, dlt, g, z):
-            nc.vector.scalar_tensor_tensor(
-                out=c_t[:, 2 * z : 2 * z + 2, :], in0=dlt[:], scalar=lam_f[:, 0:1],
-                in1=s_t[:, 4 * g + 2 * z : 4 * g + 2 * z + 2, :], op0=ALU.mult, op1=ALU.mult,
-            )
-
-        def tanh_quantise(a_t, nsg, g, m0, m1):
+        def tanh_rows(a_t, nsg, m0, m1):
             nc.scalar.activation(out=nsg[:, m0:m1, :], in_=a_t[:, :, m0:m1].rearrange("p t m -> p m t"), func=ACT.Tanh)
+
+        def quantise_rows(nsg, g, m0, m1):
             nc.vector.quantize_mx(
                 out=ns_codes[:, ROWS * g + m0 : ROWS * g + m1].bitcast(FP8X4),
                 scales=ns_scales[:, ROWS * g + m0 : ROWS * g + m1],
                 in_=nsg[:, m0:m1, :].rearrange("p m t -> p (m t)"),
             )
 
-        def group_work(g):
-            a_t = ep2.tile([P, 4, ROWS], F32, name="a_t", tag="a_t")
-            c_t = ep1.tile([P, 4, ROWS], F32, name="c_t", tag="c_t")
-            noise_b = noise_bank(g)
-            sigs = []
-            for z in range(2):
+        def group_pieces(g):
+            tiles = {}
+
+            def products(z):
                 sig = acc.tile([P, 2, ROWS], F32, name="sig", tag="sig")
                 dlt = acc.tile([P, 2, ROWS], F32, name="dlt", tag="dlt")
-                sigs.append(sig)
+                tiles[("sig", z)] = sig
+                tiles[("dlt", z)] = dlt
                 big_passes(sig, 0, g, z)
                 big_passes(dlt, 1, g, z)
-                delta_times_s(c_t, dlt, g, z)
-            for j in range(4):
+
+            def delta_times_s(z):
+                if z == 0:
+                    tiles["c"] = ep1.tile([P, 4, ROWS], F32, name="c_t", tag="c_t")
                 nc.vector.scalar_tensor_tensor(
-                    out=c_t[:, j, :], in0=noise_b[:, j // 2, :, j % 2], scalar=t01[:, 4 * g + j : 4 * g + j + 1],
-                    in1=c_t[:, j, :], op0=ALU.mult, op1=ALU.add,
+                    out=tiles["c"][:, 2 * z : 2 * z + 2, :], in0=tiles[("dlt", z)][:], scalar=lam_f[:, 0:1],
+                    in1=s_t[:, 4 * g + 2 * z : 4 * g + 2 * z + 2, :], op0=ALU.mult, op1=ALU.mult,
                 )
-            for z in range(2):
+
+            def add_noise(z):
+                for j in (2 * z, 2 * z + 1):
+                    nc.vector.scalar_tensor_tensor(
+                        out=tiles["c"][:, j, :], in0=tiles["noise"][:, z, :, j % 2],
+                        scalar=t01[:, 4 * g + j : 4 * g + j + 1],
+                        in1=tiles["c"][:, j, :], op0=ALU.mult, op1=ALU.add,
+                    )
+
+            def add_signal(z):
+                if z == 0:
+                    tiles["a"] = ep2.tile([P, 4, ROWS], F32, name="a_t", tag="a_t")
                 nc.vector.tensor_tensor(
-                    out=a_t[:, 2 * z : 2 * z + 2, :], in0=sigs[z][:], in1=c_t[:, 2 * z : 2 * z + 2, :], op=ALU.add
+                    out=tiles["a"][:, 2 * z : 2 * z + 2, :], in0=tiles[("sig", z)][:],
+                    in1=tiles["c"][:, 2 * z : 2 * z + 2, :], op=ALU.add,
                 )
-            nsg = ep2.tile([P, ROWS, 4], BF16, name="nsg", tag="nsg", align_bytes=64)
-            tanh_quantise(a_t, nsg, g, 0, ROWS)
+
+            def piece0():
+                products(0)
+
+            def piece1():
+                products(1)
+                tiles["noise"] = noise_bank(g)
+                delta_times_s(0)
+
+            def piece2():
+                delta_times_s(1)
+                add_noise(0)
+
+            def piece3():
+                add_noise(1)
+                add_signal(0)
+
+            def piece4():
+                add_signal(1)
+                tiles["ns"] = ep2.tile([P, ROWS, 4], BF16, name="nsg", tag="nsg", align_bytes=64)
+                tanh_rows(tiles["a"], tiles["ns"], 0, ROWS)
+
+            def piece5():
+                quantise_rows(tiles["ns"], g, 0, ROWS)
+
+            return [piece0, piece1, piece2, piece3, piece4, piece5]
 
         ob = {}
 
@@ -334,82 +401,109 @@ def tile_brainquantumlayer_pc_kernel(
                 stop=(g == NG - 1),
             )
 
-        def last_step(s):
-            g = NG - 1
-            a_t = ep2.tile([P, 4, ROWS], F32, name="a_t", tag="a_t")
-            c_t = ep1.tile([P, 4, ROWS], F32, name="c_t", tag="c_t")
-            unit(s, 0, 0)
-            gt, cd, sc = unit_tiles(1, 3, g)
-            for z in (1, 0):
-                regroup(gt, raw_j[s][:, :, 0:G], z, z + 1, z == 1)
-            for z in (1, 0):
-                sig = acc.tile([P, 2, ROWS], F32, name="sig", tag="sig")
-                big_passes(sig, 0, g, z)
-                for e in range(2):
-                    j = 2 * z + e
-                    nc.vector.scalar_tensor_tensor(
-                        out=a_t[:, j, :], in0=noise_3[:, z, :, e], scalar=t01[:, 4 * g + j : 4 * g + j + 1],
-                        in1=sig[:, e, :], op0=ALU.mult, op1=ALU.add,
-                    )
-            dlts = {}
-            for j in (2, 3, 0, 1):
-                tag = "dlt" if j >= 2 else "sig"
-                dlts[j] = acc.tile([P, 2, ROWS], F32, name=tag, tag=tag)
-                for kp in range(3):
-                    block_pass(dlts[j][:, 0, :], 1, g, j, kp)
-            for z in (1, 0):
-                quantise(gt, cd, sc, z, z + 1)
-                for j in (2 * z, 2 * z + 1):
-                    block_pass(dlts[j][:, 0, :], 1, g, j, 3)
-            for z in (1, 0):
-                for j in (2 * z, 2 * z + 1):
-                    nc.vector.scalar_tensor_tensor(
-                        out=c_t[:, j, :], in0=dlts[j][:, 0, :], scalar=lam_f[:, 0:1],
-                        in1=s_t[:, 4 * g + j, :], op0=ALU.mult, op1=ALU.mult,
-                    )
-                zz = slice(2 * z, 2 * z + 2)
-                nc.vector.tensor_tensor(out=a_t[:, zz, :], in0=a_t[:, zz, :], in1=c_t[:, zz, :], op=ALU.add)
-            nsg = ep2.tile([P, ROWS, 4], BF16, name="nsg", tag="nsg", align_bytes=64)
+        def out_open(oc):
             for mt in range(2):
-                tanh_quantise(a_t, nsg, g, P * mt, P * mt + P)
-                o_sb = ep2.tile([P, D_OUT], F32, name="a_t", tag="a_t")
-                for oc in range(2):
+                ob[(mt, oc)] = trp.tile([P, 512], F32, name="tr", tag="tr")
+            for g in range(NG - 1):
+                for mt in range(2):
                     out_pass(g, mt, oc)
-                    cols = slice(512 * oc, 512 * oc + 512)
-                    nc.vector.tensor_tensor(out=o_sb[:, cols], in0=ob[(mt, oc)][:], in1=bias[:, cols], op=ALU.add)
-                    nc.sync.dma_start(out=out[P * mt : P * mt + P, cols], in_=o_sb[:, cols])
 
-        WO_LOAD = {1: 0, 2: 1, 4: 2, 5: 3}
-        WO_WORK = {4: 0, 5: 1, 7: 2, 8: 3}
-        multiply_both(0)
-        for s in range(n_steps):
-            g0, ng, kp = steps[s]
-            if s + 1 < n_steps:
-                multiply_both(s + 1)
-            if s == n_steps - 1:
-                last_step(s)
-                break
-            for kind in range(2):
-                for h in range(ng):
-                    unit(s, kind, h)
-            load_mask(s + 3)
-            load_wj(s + 3)
-            if s == 0:
-                noise_load()
-            if s in WO_LOAD:
-                wo_load(WO_LOAD[s])
-            if s in WO_WORK:
-                wo_work(WO_WORK[s])
-            if s == 7:
-                noise_last()
-            if kp == 3:
-                for g in range(g0, g0 + ng):
-                    group_work(g)
-                if g0 + ng == NG - 1:
-                    for mt in range(2):
-                        for oc in range(2):
-                            ob[(mt, oc)] = trp.tile([P, 512], F32, name="tr", tag="tr")
-                    for gg in range(NG - 1):
-                        for mt in range(2):
-                            for oc in range(2):
-                                out_pass(gg, mt, oc)
+        plan = {}
+
+        def weave(start, pieces, every=1):
+            for i, piece in enumerate(pieces):
+                plan.setdefault(start + every * i, []).append(piece)
+
+        def pair(fn, *args):
+            return lambda: fn(*args)
+
+        def run_all(pieces):
+            for piece in pieces:
+                piece()
+
+        weave(3, [pair(state_gather, 0), pair(state_gather, 1), pair(state_tanh, 0), pair(state_tanh, 1)])
+        weave(6, [pair(state_round, 0), pair(state_quantise, 0), pair(state_round, 1), pair(state_quantise, 1)])
+        for q, start in ((0, 9), (1, 12), (2, 24)):
+            for gp in range(2):
+                weave(start + 2 * gp, [pair(wo_gather, q, gp), pair(wo_quantise, q, gp)])
+        last_unit = {g: units.index((1, 3, g)) for g in range(NG)}
+        weave(last_unit[0] + QUANT_LAG, group_pieces(0))
+        weave(last_unit[1] + QUANT_LAG + 1, group_pieces(1))
+        two = group_pieces(2)
+        weave(last_unit[2] + QUANT_LAG, [pair(run_all, two[0:2]), pair(run_all, two[2:4]), two[4]])
+        weave(last_unit[2] + QUANT_LAG - 1, [noise_last])
+
+        for u in range(MULT_LEAD):
+            multiply_for(u)
+        for u in range(n_units):
+            regroup(u)
+            if on_pe(u + 1):
+                interleave_on_pe(u + 1)
+            quantise(u - QUANT_LAG)
+            last_of_step = u + 1 == n_units or unit_step[u + 1] != unit_step[u]
+            if last_of_step:
+                s = unit_step[u]
+                load_step(s + 3)
+                if s == 3:
+                    noise_load()
+                if s in (1, 2, 5, 6):
+                    wo_load((1, 2, 5, 6).index(s))
+            for piece in plan.get(u, ()):
+                piece()
+            multiply_for(u + MULT_LEAD)
+
+        g = NG - 1
+        last = n_units - 1
+        a_t = ep2.tile([P, 4, ROWS], F32, name="a_t", tag="a_t")
+        c_t = ep1.tile([P, 4, ROWS], F32, name="c_t", tag="c_t")
+        for gp in range(2):
+            wo_gather(3, gp)
+        quantise(last - 1)
+        for z in (1, 0):
+            sig = acc.tile([P, 2, ROWS], F32, name="sig", tag="sig")
+            big_passes(sig, 0, g, z)
+            for e in range(2):
+                j = 2 * z + e
+                nc.vector.scalar_tensor_tensor(
+                    out=a_t[:, j, :], in0=noise_3[:, z, :, e], scalar=t01[:, 4 * g + j : 4 * g + j + 1],
+                    in1=sig[:, e, :], op0=ALU.mult, op1=ALU.add,
+                )
+        two[5]()
+        code_tiles(last)
+        dlts = {}
+        for j in (2, 3, 0, 1):
+            tag = "dlt" if j >= 2 else "sig"
+            dlts[j] = acc.tile([P, 2, ROWS], F32, name=tag, tag=tag)
+            for kp in range(3):
+                block_pass(dlts[j][:, 0, :], 1, g, j, kp)
+        for z in (1, 0):
+            quantise_part(last, z, z + 1)
+            for j in (2 * z, 2 * z + 1):
+                block_pass(dlts[j][:, 0, :], 1, g, j, 3)
+        for gp in range(2):
+            wo_quantise(3, gp)
+        for z in (1, 0):
+            for j in (2 * z, 2 * z + 1):
+                nc.vector.scalar_tensor_tensor(
+                    out=c_t[:, j, :], in0=dlts[j][:, 0, :], scalar=lam_f[:, 0:1],
+                    in1=s_t[:, 4 * g + j, :], op0=ALU.mult, op1=ALU.mult,
+                )
+        for z in (1, 0):
+            zz = slice(2 * z, 2 * z + 2)
+            nc.vector.tensor_tensor(out=a_t[:, zz, :], in0=a_t[:, zz, :], in1=c_t[:, zz, :], op=ALU.add)
+        nsg = ep2.tile([P, ROWS, 4], BF16, name="nsg", tag="nsg", align_bytes=64)
+        for mt in range(2):
+            tanh_rows(a_t, nsg, P * mt, P * mt + P)
+        out_open(0)
+        out_open(1)
+        o_sb = natp.tile([P, 4, 512], F32, name="nat", tag="nat")
+        for mt in range(2):
+            quantise_rows(nsg, g, P * mt, P * mt + P)
+            for oc in range(2):
+                out_pass(g, mt, oc)
+        for mt in range(2):
+            for oc in range(2):
+                cols = slice(512 * oc, 512 * oc + 512)
+                o_part = o_sb[:, 2 * mt + oc, :]
+                nc.vector.tensor_tensor(out=o_part, in0=ob[(mt, oc)][:], in1=bias[:, cols], op=ALU.add)
+                nc.sync.dma_start(out=out[P * mt : P * mt + P, cols], in_=o_part)

@@ -241,8 +241,8 @@ def tile_brainquantumlayer_pc_kernel(
             return raw[(kind, unit_step[u])][:, :, G * h : G * h + G]
 
         def regroup_part(gt, src, z0, z1, on_vector):
-            dst = gt[:].rearrange("p (i c t) -> p c t i", i=4, t=4)[:, :, :, 2 * z0 : 2 * z1]
-            srcv = src.rearrange("p t (c i) -> p c t i", i=4)[:, :, :, 2 * z0 : 2 * z1]
+            dst = gt[:].rearrange("p (i c t) -> p c i t", i=4, t=4)[:, :, 2 * z0 : 2 * z1, :]
+            srcv = src.rearrange("p t (c i) -> p c i t", i=4)[:, :, 2 * z0 : 2 * z1, :]
             if on_vector:
                 nc.vector.tensor_copy(out=dst, in_=srcv)
             else:

@@ -21,16 +21,14 @@ G = 512
 NG = NEUR // G
 FLOPS = 2 * ROWS * NEUR * NEUR * 2 + 2 * ROWS * NEUR * D_OUT
 
-STEPS = (
-    (0, 1, 0), (1, 1, 0), (0, 1, 1), (1, 1, 1), (0, 2, 2), (0, 2, 3),
-    (2, 2, 0), (2, 2, 1), (2, 1, 2), (2, 1, 3), (3, 1, 2), (3, 1, 3),
-)
 PE_EVERY = 4
-PE_MAX = 7
-V_EVERY = 16
-V_PHASE = 9
-MULT_LEAD = 2
+PE_MAX = 0
+V_EVERY = 7
+V_PHASE = 4
+LOAD_LEAD = 10
+MULT_LEAD = 3
 QUANT_LAG = 2
+PE_LEAD = 2
 PI_HI = 3.1415927410125732
 PI_LO = math.pi - PI_HI
 
@@ -42,10 +40,10 @@ def tile_brainquantumlayer_pc_kernel(
     with ExitStack() as ctx:
         const = ctx.enter_context(tc.tile_pool(name="const", bufs=1))
         natp = ctx.enter_context(tc.tile_pool(name="natp", bufs=2))
-        mpool = ctx.enter_context(tc.tile_pool(name="mpool", bufs=3))
-        wpool = ctx.enter_context(tc.tile_pool(name="wpool", bufs=3))
-        grp = ctx.enter_context(tc.tile_pool(name="grp", bufs=5))
-        cpool = ctx.enter_context(tc.tile_pool(name="cpool", bufs=10))
+        mpool = ctx.enter_context(tc.tile_pool(name="mpool", bufs=5))
+        wpool = ctx.enter_context(tc.tile_pool(name="wpool", bufs=11))
+        grp = ctx.enter_context(tc.tile_pool(name="grp", bufs=8))
+        cpool = ctx.enter_context(tc.tile_pool(name="cpool", bufs=7))
         ep2 = ctx.enter_context(tc.tile_pool(name="ep2", bufs=2))
         ep1 = ctx.enter_context(tc.tile_pool(name="ep1", bufs=1))
         acc = ctx.enter_context(tc.psum_pool(name="acc", bufs=2))
@@ -58,29 +56,24 @@ def tile_brainquantumlayer_pc_kernel(
         wo_v = W_out.rearrange("(q t p) n -> q p t n", t=2, p=P)
 
         units = []
-        unit_step = []
-        for s, (g0, ng, kp) in enumerate(STEPS):
-            by_group = [(kind, kp, g0 + h) for h in range(ng) for kind in range(2)]
-            by_kind = [(kind, kp, g0 + h) for kind in range(2) for h in range(ng)]
-            order = by_group if kp == 3 else by_kind
-            units.extend(order)
-            unit_step.extend([s] * len(order))
+        for g in range(NG - 1):
+            units.extend((kind, kp, g) for kp in range(4) for kind in range(2))
+        units.extend((kind, kp, NG - 1) for kind in range(2) for kp in range(4))
         n_units = len(units)
         raw_m = {}
         raw = {}
 
-        def load_step(s):
-            if s < len(STEPS):
-                g0, ng, kp = STEPS[s]
-                cols = slice(G * g0, G * (g0 + ng))
-                t = mpool.tile([P, 4, G * ng], BF16, name="m_raw", tag="m_raw")
-                nc.sync.dma_start(out=t[:], in_=m_v[kp, :, :, cols])
-                raw_m[s] = t
-                for kind, view in ((0, w_v), (1, j_v)):
-                    name = "w_raw" if kind == 0 else "j_raw"
-                    t = wpool.tile([P, 4, G * ng], BF16, name=name, tag=name)
-                    nc.sync.dma_start(out=t[:], in_=view[kp, :, :, cols])
-                    raw[(kind, s)] = t
+        def load_unit(u):
+            if u < n_units:
+                kind, kp, g = units[u]
+                cols = slice(G * g, G * g + G)
+                if (kp, g) not in raw_m:
+                    t = mpool.tile([P, 4, G], BF16, name="m_raw", tag="m_raw")
+                    nc.sync.dma_start(out=t[:], in_=m_v[kp, :, :, cols])
+                    raw_m[(kp, g)] = t
+                t = wpool.tile([P, 4, G], BF16, name="raw", tag="raw")
+                nc.sync.dma_start(out=t[:], in_=(w_v, j_v)[kind][kp, :, :, cols])
+                raw[u] = t
 
         wo_nat = {}
 
@@ -96,12 +89,13 @@ def tile_brainquantumlayer_pc_kernel(
         brow = grp.tile([P, D_OUT], BF16, name="grp", tag="grp", align_bytes=64)
         nc.gpsimd.memset(brow[:], 0.0)
         nc.scalar.dma_start(out=brow[0:1, :], in_=b_out.unsqueeze(0))
-        load_step(0)
-        load_step(1)
+        for u in range(7):
+            load_unit(u)
         st_nat = natp.tile([P, 2, NEUR], BF16, name="nat", tag="nat")
         for t in range(2):
             nc.sync.dma_start(out=st_nat[:, t, :], in_=state[P * t : P * t + P, :])
-        load_step(2)
+        for u in range(7, LOAD_LEAD):
+            load_unit(u)
         nz_nat = const.tile([P, 2, NEUR], BF16, name="nz_nat")
 
         ident = const.tile([P, P], F32, name="ident")
@@ -154,13 +148,17 @@ def tile_brainquantumlayer_pc_kernel(
         stgs = {}
         sgs = {}
 
+        state_banks = {}
+
+        def state_transpose(gp):
+            for gl in range(2):
+                state_banks[2 * gp + gl] = transposed_bank(word_view(st_nat), 2 * gp + gl)
+
         def state_gather(gp):
-            words = word_view(st_nat)
             stg = grp.tile([P, 2048], BF16, name="grp", tag="grp", align_bytes=64)
             stg_w = stg[:].bitcast(F32).rearrange("p (g m z) -> p g m z", g=2, z=2)
             for gl in range(2):
-                bank = transposed_bank(words, 2 * gp + gl)
-                nc.vector.tensor_copy(out=stg_w[:, gl], in_=bank[:].rearrange("p z m -> p m z"))
+                nc.vector.tensor_copy(out=stg_w[:, gl], in_=state_banks[2 * gp + gl][:].rearrange("p z m -> p m z"))
             stgs[gp] = stg
 
         def state_half(gp):
@@ -192,8 +190,13 @@ def tile_brainquantumlayer_pc_kernel(
         def noise_load():
             nc.sync.dma_start(out=nz_nat[:], in_=noise_raw.rearrange("(t p) k -> p t k", p=P))
 
+        noise_last_bank = []
+
+        def noise_transpose_last():
+            noise_last_bank.append(transposed_bank(word_view(nz_nat), NG - 1))
+
         def noise_last():
-            bank = transposed_bank(word_view(nz_nat), NG - 1)
+            bank = noise_last_bank[0]
             nc.scalar.copy(out=noise_3[:].rearrange("p z m e -> p (z m e)").bitcast(F32), in_=bank[:].rearrange("p z m -> p (z m)"))
 
         def noise_bank(g):
@@ -204,12 +207,17 @@ def tile_brainquantumlayer_pc_kernel(
         wo_scales = const.tile([P, NG, D_OUT], U8, name="wo_scales", align_bytes=64)
         wo_gt = {}
 
+        wo_banks = {}
+
+        def wo_transpose(q, gp):
+            for gl in range(2):
+                wo_banks[(q, 2 * gp + gl)] = transposed_bank(word_view(wo_nat[q]), 2 * gp + gl)
+
         def wo_gather(q, gp):
             gt = grp.tile([P, 2048], BF16, name="grp", tag="grp", align_bytes=64)
             gw = gt[:].bitcast(F32).rearrange("p (g o z) -> p g o z", g=2, z=2)
             for gl in range(2):
-                bank = transposed_bank(word_view(wo_nat[q]), 2 * gp + gl)
-                nc.scalar.copy(out=gw[:, gl], in_=bank[:].rearrange("p z o -> p o z"))
+                nc.scalar.copy(out=gw[:, gl], in_=wo_banks[(q, 2 * gp + gl)][:].rearrange("p z o -> p o z"))
             wo_gt[(q, gp)] = gt
 
         def wo_quantise(q, gp):
@@ -225,20 +233,14 @@ def tile_brainquantumlayer_pc_kernel(
         ns_scales = const.tile([P, NG * ROWS], U8, name="ns_scales", align_bytes=64)
         codes = {}
         gts = {}
-        multiplied = set()
 
         def multiply_for(u):
             if u < n_units:
-                key = (units[u][0], unit_step[u])
-                if key not in multiplied:
-                    multiplied.add(key)
-                    t = raw[key]
-                    nc.vector.tensor_tensor(out=t[:], in0=t[:], in1=raw_m[key[1]][:], op=ALU.mult)
+                kind, kp, g = units[u]
+                nc.vector.tensor_tensor(out=raw[u][:], in0=raw[u][:], in1=raw_m[(kp, g)][:], op=ALU.mult)
 
         def source(u):
-            kind, kp, g = units[u]
-            h = g - STEPS[unit_step[u]][0]
-            return raw[(kind, unit_step[u])][:, :, G * h : G * h + G]
+            return raw[u][:]
 
         def regroup_part(gt, src, z0, z1, on_vector):
             dst = gt[:].rearrange("p (i c t) -> p c i t", i=4, t=4)[:, :, 2 * z0 : 2 * z1, :]
@@ -326,6 +328,9 @@ def tile_brainquantumlayer_pc_kernel(
                 in_=nsg[:, m0:m1, :].rearrange("p m t -> p (m t)"),
             )
 
+        def pair(fn, *args):
+            return lambda: fn(*args)
+
         def group_pieces(g):
             tiles = {}
 
@@ -361,31 +366,26 @@ def tile_brainquantumlayer_pc_kernel(
                     in1=tiles["c"][:, 2 * z : 2 * z + 2, :], op=ALU.add,
                 )
 
-            def piece0():
-                products(0)
-
-            def piece1():
-                products(1)
+            def transpose_noise():
                 tiles["noise"] = noise_bank(g)
-                delta_times_s(0)
 
-            def piece2():
-                delta_times_s(1)
-                add_noise(0)
-
-            def piece3():
-                add_noise(1)
-                add_signal(0)
-
-            def piece4():
-                add_signal(1)
+            def tanh():
                 tiles["ns"] = ep2.tile([P, ROWS, 4], BF16, name="nsg", tag="nsg", align_bytes=64)
                 tanh_rows(tiles["a"], tiles["ns"], 0, ROWS)
 
-            def piece5():
+            def last():
                 quantise_rows(tiles["ns"], g, 0, ROWS)
 
-            return [piece0, piece1, piece2, piece3, piece4, piece5]
+            return [
+                [pair(products, 0)],
+                [pair(products, 1), transpose_noise],
+                [],
+                [pair(delta_times_s, 0)],
+                [pair(delta_times_s, 1), pair(add_noise, 0)],
+                [pair(add_noise, 1), pair(add_signal, 0)],
+                [pair(add_signal, 1), tanh],
+                [last],
+            ]
 
         ob = {}
 
@@ -401,87 +401,92 @@ def tile_brainquantumlayer_pc_kernel(
                 stop=(g == NG - 1),
             )
 
-        def out_open(oc):
+        def out_add(g):
             for mt in range(2):
-                ob[(mt, oc)] = trp.tile([P, 512], F32, name="tr", tag="tr")
-            for g in range(NG - 1):
-                for mt in range(2):
+                for oc in range(2):
+                    if g == 0:
+                        ob[(mt, oc)] = trp.tile([P, 512], F32, name="tr", tag="tr")
                     out_pass(g, mt, oc)
+
+        last = n_units - 1
+        last_tiles = {}
+
+        def last_signal(z):
+            if z == 1:
+                last_tiles["a"] = ep2.tile([P, 4, ROWS], F32, name="a_t", tag="a_t")
+            last_tiles[z] = acc.tile([P, 2, ROWS], F32, name="sig", tag="sig")
+            big_passes(last_tiles[z], 0, NG - 1, z)
+
+        def last_noise_add(z):
+            for e in range(2):
+                j = 2 * z + e
+                nc.vector.scalar_tensor_tensor(
+                    out=last_tiles["a"][:, j, :], in0=noise_3[:, z, :, e],
+                    scalar=t01[:, 4 * (NG - 1) + j : 4 * (NG - 1) + j + 1],
+                    in1=last_tiles[z][:, e, :], op0=ALU.mult, op1=ALU.add,
+                )
 
         plan = {}
 
-        def weave(start, pieces, every=1):
-            for i, piece in enumerate(pieces):
-                plan.setdefault(start + every * i, []).append(piece)
+        def weave(start, pieces):
+            for i, group in enumerate(pieces):
+                plan.setdefault(start + i, []).extend(group)
 
-        def pair(fn, *args):
-            return lambda: fn(*args)
-
-        def run_all(pieces):
+        def run(pieces):
             for piece in pieces:
                 piece()
 
-        weave(3, [pair(state_gather, 0), pair(state_gather, 1), pair(state_tanh, 0), pair(state_tanh, 1)])
-        weave(6, [pair(state_round, 0), pair(state_quantise, 0), pair(state_round, 1), pair(state_quantise, 1)])
-        for q, start in ((0, 9), (1, 12), (2, 24)):
+        for gp in range(2):
+            weave(5 + gp, [
+                [pair(state_transpose, gp)], [pair(state_gather, gp)], [pair(state_tanh, gp)],
+                [], [pair(state_round, gp)], [pair(state_quantise, gp)],
+            ])
+        for q, start in enumerate((14, 17, 22, 26)):
             for gp in range(2):
-                weave(start + 2 * gp, [pair(wo_gather, q, gp), pair(wo_quantise, q, gp)])
+                weave(start + 2 * gp, [[pair(wo_transpose, q, gp)], [pair(wo_gather, q, gp)], [pair(wo_quantise, q, gp)]])
         last_unit = {g: units.index((1, 3, g)) for g in range(NG)}
-        weave(last_unit[0] + QUANT_LAG, group_pieces(0))
-        weave(last_unit[1] + QUANT_LAG + 1, group_pieces(1))
-        two = group_pieces(2)
-        weave(last_unit[2] + QUANT_LAG, [pair(run_all, two[0:2]), pair(run_all, two[2:4]), two[4]])
-        weave(last_unit[2] + QUANT_LAG - 1, [noise_last])
+        for g in range(NG - 1):
+            pieces = group_pieces(g)
+            if g == NG - 2:
+                pieces.remove([])
+            weave(last_unit[g] + QUANT_LAG + (3 if g == 0 else 0), pieces)
+        weave(last_unit[NG - 2] + 1, [[noise_transpose_last], [noise_last]])
+        weave(n_units - 2, [[pair(last_signal, 1)], [pair(last_signal, 0)]])
 
         for u in range(MULT_LEAD):
             multiply_for(u)
         for u in range(n_units):
             regroup(u)
-            if on_pe(u + 1):
-                interleave_on_pe(u + 1)
             quantise(u - QUANT_LAG)
-            last_of_step = u + 1 == n_units or unit_step[u + 1] != unit_step[u]
-            if last_of_step:
-                s = unit_step[u]
-                load_step(s + 3)
-                if s == 3:
-                    noise_load()
-                if s in (1, 2, 5, 6):
-                    wo_load((1, 2, 5, 6).index(s))
-            for piece in plan.get(u, ()):
-                piece()
+            load_unit(u + LOAD_LEAD)
+            if u == 3:
+                noise_load()
+            if u in (5, 9, 13, 17):
+                wo_load((5, 9, 13, 17).index(u))
+            run(plan.get(u, ()))
             multiply_for(u + MULT_LEAD)
 
-        g = NG - 1
-        last = n_units - 1
-        a_t = ep2.tile([P, 4, ROWS], F32, name="a_t", tag="a_t")
-        c_t = ep1.tile([P, 4, ROWS], F32, name="c_t", tag="c_t")
-        for gp in range(2):
-            wo_gather(3, gp)
         quantise(last - 1)
         for z in (1, 0):
-            sig = acc.tile([P, 2, ROWS], F32, name="sig", tag="sig")
-            big_passes(sig, 0, g, z)
-            for e in range(2):
-                j = 2 * z + e
-                nc.vector.scalar_tensor_tensor(
-                    out=a_t[:, j, :], in0=noise_3[:, z, :, e], scalar=t01[:, 4 * g + j : 4 * g + j + 1],
-                    in1=sig[:, e, :], op0=ALU.mult, op1=ALU.add,
-                )
-        two[5]()
+            last_noise_add(z)
         code_tiles(last)
+        g = NG - 1
+        a_t = last_tiles["a"]
+        c_t = ep1.tile([P, 4, ROWS], F32, name="c_t", tag="c_t")
         dlts = {}
         for j in (2, 3, 0, 1):
             tag = "dlt" if j >= 2 else "sig"
             dlts[j] = acc.tile([P, 2, ROWS], F32, name=tag, tag=tag)
             for kp in range(3):
                 block_pass(dlts[j][:, 0, :], 1, g, j, kp)
+        for u in sorted(plan):
+            if u >= n_units:
+                run(plan[u])
+        out_add(0)
         for z in (1, 0):
             quantise_part(last, z, z + 1)
             for j in (2 * z, 2 * z + 1):
                 block_pass(dlts[j][:, 0, :], 1, g, j, 3)
-        for gp in range(2):
-            wo_quantise(3, gp)
         for z in (1, 0):
             for j in (2 * z, 2 * z + 1):
                 nc.vector.scalar_tensor_tensor(
@@ -494,8 +499,8 @@ def tile_brainquantumlayer_pc_kernel(
         nsg = ep2.tile([P, ROWS, 4], BF16, name="nsg", tag="nsg", align_bytes=64)
         for mt in range(2):
             tanh_rows(a_t, nsg, P * mt, P * mt + P)
-        out_open(0)
-        out_open(1)
+        out_add(1)
+        out_add(2)
         o_sb = natp.tile([P, 4, 512], F32, name="nat", tag="nat")
         for mt in range(2):
             quantise_rows(nsg, g, P * mt, P * mt + P)

@@ -21,14 +21,11 @@ G = 512
 NG = NEUR // G
 FLOPS = 2 * ROWS * NEUR * NEUR * 2 + 2 * ROWS * NEUR * D_OUT
 
-PE_EVERY = 4
-PE_MAX = 0
 V_EVERY = 7
 V_PHASE = 4
 LOAD_LEAD = 10
 MULT_LEAD = 3
 QUANT_LAG = 2
-PE_LEAD = 2
 PI_HI = 3.1415927410125732
 PI_LO = math.pi - PI_HI
 
@@ -41,7 +38,8 @@ def tile_brainquantumlayer_pc_kernel(
         const = ctx.enter_context(tc.tile_pool(name="const", bufs=1))
         natp = ctx.enter_context(tc.tile_pool(name="natp", bufs=2))
         mpool = ctx.enter_context(tc.tile_pool(name="mpool", bufs=5))
-        wpool = ctx.enter_context(tc.tile_pool(name="wpool", bufs=11))
+        wpool = ctx.enter_context(tc.tile_pool(name="wpool", bufs=8))
+        ppool = ctx.enter_context(tc.tile_pool(name="ppool", bufs=5))
         grp = ctx.enter_context(tc.tile_pool(name="grp", bufs=8))
         cpool = ctx.enter_context(tc.tile_pool(name="cpool", bufs=7))
         ep2 = ctx.enter_context(tc.tile_pool(name="ep2", bufs=2))
@@ -100,8 +98,6 @@ def tile_brainquantumlayer_pc_kernel(
 
         ident = const.tile([P, P], F32, name="ident")
         make_identity(nc, ident[:])
-        ident_bf = const.tile([P, P], BF16, name="ident_bf")
-        make_identity(nc, ident_bf[:])
         ones = const.tile([P, P], BF16, name="ones")
         nc.vector.memset(ones[:], 1.0)
         lam_f = const.tile([P, 1], F32, name="lam_f")
@@ -124,10 +120,12 @@ def tile_brainquantumlayer_pc_kernel(
         nc.scalar.activation(out=t01[:], in_=sn[:], func=ACT.Abs, scale=0.1)
 
         bias = const.tile([P, D_OUT], BF16, name="bias")
-        for oc in range(2):
-            pb = trp.tile([P, 512], F32, name="tr", tag="tr")
-            nc.tensor.matmul(out=pb[:], lhsT=ones[:], rhs=brow[:, 512 * oc : 512 * oc + 512], start=True, stop=True)
-            nc.scalar.copy(out=bias[:, 512 * oc : 512 * oc + 512], in_=pb[:])
+
+        def bias_spread():
+            for oc in range(2):
+                pb = trp.tile([P, 512], F32, name="tr", tag="tr")
+                nc.tensor.matmul(out=pb[:], lhsT=ones[:], rhs=brow[:, 512 * oc : 512 * oc + 512], start=True, stop=True)
+                nc.scalar.copy(out=bias[:, 512 * oc : 512 * oc + 512], in_=pb[:])
 
         st_codes = const.tile([P, 4 * ROWS], U32, name="st_codes", align_bytes=64)
         st_scales = const.tile([P, 4 * ROWS], U8, name="st_scales", align_bytes=64)
@@ -234,51 +232,35 @@ def tile_brainquantumlayer_pc_kernel(
         codes = {}
         gts = {}
 
+        product = {}
+
         def multiply_for(u):
             if u < n_units:
                 kind, kp, g = units[u]
-                nc.vector.tensor_tensor(out=raw[u][:], in0=raw[u][:], in1=raw_m[(kp, g)][:], op=ALU.mult)
+                product[u] = ppool.tile([P, P, 4, 4], BF16, name="product", tag="product")
+                nc.vector.tensor_tensor(
+                    out=product[u][:],
+                    in0=raw[u][:].rearrange("p t (q i) -> p q t i", i=4),
+                    in1=raw_m[(kp, g)][:].rearrange("p t (q i) -> p q t i", i=4),
+                    op=ALU.mult,
+                )
 
-        def source(u):
-            return raw[u][:]
-
-        def regroup_part(gt, src, z0, z1, on_vector):
-            dst = gt[:].rearrange("p (i c t) -> p c i t", i=4, t=4)[:, :, 2 * z0 : 2 * z1, :]
-            srcv = src.rearrange("p t (c i) -> p c i t", i=4)[:, :, 2 * z0 : 2 * z1, :]
+        def regroup_part(gt, u, z0, z1, on_vector):
+            dst = gt[:].rearrange("p (i h r) -> p h i r", i=4, r=8)[:, :, 2 * z0 : 2 * z1, :]
+            srcv = product[u][:].rearrange("p (h d) t i -> p h i (d t)", d=2)[:, :, 2 * z0 : 2 * z1, :]
             if on_vector:
                 nc.vector.tensor_copy(out=dst, in_=srcv)
             else:
                 nc.scalar.copy(out=dst, in_=srcv)
 
-        pe_banks = {}
-
-        def on_pe(u):
-            return u % PE_EVERY == PE_EVERY - 1 and u // PE_EVERY < PE_MAX
-
-        def interleave_on_pe(u):
-            src = source(u)
-            for z in range(2):
-                bank = trp.tile([P, 2, P, 4], BF16, name="tr", tag="tr")
-                pe_banks[(u, z)] = bank
-                for i in range(2):
-                    nc.tensor.matmul(
-                        out=bank[:, i, :, :], lhsT=ident_bf[:],
-                        rhs=src.rearrange("p t (c i) -> p i c t", i=4)[:, 2 * z + i, :, :],
-                        start=True, stop=True,
-                    )
-
         def regroup(u):
             gt = grp.tile([P, 2048], BF16, name="grp", tag="grp", align_bytes=64)
             gts[u] = gt
-            if on_pe(u):
-                for z in range(2):
-                    half = slice(1024 * z, 1024 * z + 1024)
-                    nc.scalar.copy(out=gt[:, half], in_=pe_banks[(u, z)][:].rearrange("p i c t -> p (i c t)"))
-            elif u == n_units - 1:
+            if u == n_units - 1:
                 for z in (1, 0):
-                    regroup_part(gt, source(u), z, z + 1, z == 1)
+                    regroup_part(gt, u, z, z + 1, z == 1)
             else:
-                regroup_part(gt, source(u), 0, 2, u % V_EVERY == V_PHASE)
+                regroup_part(gt, u, 0, 2, u % V_EVERY == V_PHASE)
 
         def code_tiles(u):
             kind = units[u][0]
@@ -452,6 +434,8 @@ def tile_brainquantumlayer_pc_kernel(
             weave(last_unit[g] + QUANT_LAG + (3 if g == 0 else 0), pieces)
         weave(last_unit[NG - 2] + 1, [[noise_transpose_last], [noise_last]])
         weave(n_units - 2, [[pair(last_signal, 1)], [pair(last_signal, 0)]])
+
+        weave(3, [[bias_spread]])
 
         for u in range(MULT_LEAD):
             multiply_for(u)

@@ -21,8 +21,8 @@ G = 512
 NG = NEUR // G
 FLOPS = 2 * ROWS * NEUR * NEUR * 2 + 2 * ROWS * NEUR * D_OUT
 
-V_EVERY = 7
-V_PHASE = 4
+V_EVERY = 6
+V_PHASE = 3
 LOAD_LEAD = 10
 MULT_LEAD = 3
 QUANT_LAG = 2
@@ -87,13 +87,12 @@ def tile_brainquantumlayer_pc_kernel(
         brow = grp.tile([P, D_OUT], BF16, name="grp", tag="grp", align_bytes=64)
         nc.gpsimd.memset(brow[:], 0.0)
         nc.scalar.dma_start(out=brow[0:1, :], in_=b_out.unsqueeze(0))
-        for u in range(7):
-            load_unit(u)
         st_nat = natp.tile([P, 2, NEUR], BF16, name="nat", tag="nat")
-        for t in range(2):
-            nc.sync.dma_start(out=st_nat[:, t, :], in_=state[P * t : P * t + P, :])
-        for u in range(7, LOAD_LEAD):
+        for u in range(LOAD_LEAD):
             load_unit(u)
+            if u in (3, 5):
+                t = (3, 5).index(u)
+                nc.sync.dma_start(out=st_nat[:, t, :], in_=state[P * t : P * t + P, :])
         nz_nat = const.tile([P, 2, NEUR], BF16, name="nz_nat")
 
         ident = const.tile([P, P], F32, name="ident")
@@ -256,11 +255,7 @@ def tile_brainquantumlayer_pc_kernel(
         def regroup(u):
             gt = grp.tile([P, 2048], BF16, name="grp", tag="grp", align_bytes=64)
             gts[u] = gt
-            if u == n_units - 1:
-                for z in (1, 0):
-                    regroup_part(gt, u, z, z + 1, z == 1)
-            else:
-                regroup_part(gt, u, 0, 2, u % V_EVERY == V_PHASE)
+            regroup_part(gt, u, 0, 2, u % V_EVERY == V_PHASE or u == n_units - 1)
 
         def code_tiles(u):
             kind = units[u][0]
@@ -419,7 +414,7 @@ def tile_brainquantumlayer_pc_kernel(
                 piece()
 
         for gp in range(2):
-            weave(5 + gp, [
+            weave(4 + gp, [
                 [pair(state_transpose, gp)], [pair(state_gather, gp)], [pair(state_tanh, gp)],
                 [], [pair(state_round, gp)], [pair(state_quantise, gp)],
             ])
@@ -430,18 +425,22 @@ def tile_brainquantumlayer_pc_kernel(
         for g in range(NG - 1):
             pieces = group_pieces(g)
             if g == NG - 2:
-                pieces.remove([])
+                p = pieces
+                pieces = [p[0] + p[1], [], p[3] + p[4], p[5], p[6], [], p[7]]
             weave(last_unit[g] + QUANT_LAG + (3 if g == 0 else 0), pieces)
         weave(last_unit[NG - 2] + 1, [[noise_transpose_last], [noise_last]])
-        weave(n_units - 2, [[pair(last_signal, 1)], [pair(last_signal, 0)]])
+        weave(n_units - 2, [[pair(last_signal, 1), pair(last_signal, 0)], [pair(last_noise_add, 1), pair(last_noise_add, 0)]])
 
         weave(3, [[bias_spread]])
 
         for u in range(MULT_LEAD):
             multiply_for(u)
         for u in range(n_units):
-            regroup(u)
+            if u < n_units - 1:
+                regroup(u)
             quantise(u - QUANT_LAG)
+            if u == n_units - 2:
+                regroup(n_units - 1)
             load_unit(u + LOAD_LEAD)
             if u == 3:
                 noise_load()
@@ -450,10 +449,9 @@ def tile_brainquantumlayer_pc_kernel(
             run(plan.get(u, ()))
             multiply_for(u + MULT_LEAD)
 
-        quantise(last - 1)
-        for z in (1, 0):
-            last_noise_add(z)
-        code_tiles(last)
+        for u in sorted(plan):
+            if u >= n_units:
+                run(plan[u])
         g = NG - 1
         a_t = last_tiles["a"]
         c_t = ep1.tile([P, 4, ROWS], F32, name="c_t", tag="c_t")
@@ -461,16 +459,14 @@ def tile_brainquantumlayer_pc_kernel(
         for j in (2, 3, 0, 1):
             tag = "dlt" if j >= 2 else "sig"
             dlts[j] = acc.tile([P, 2, ROWS], F32, name=tag, tag=tag)
-            for kp in range(3):
+            for kp in range(2):
                 block_pass(dlts[j][:, 0, :], 1, g, j, kp)
-        for u in sorted(plan):
-            if u >= n_units:
-                run(plan[u])
+        quantise(last)
+        quantise(last - 1)
+        for j in (2, 3, 0, 1):
+            for kp in (2, 3):
+                block_pass(dlts[j][:, 0, :], 1, g, j, kp)
         out_add(0)
-        for z in (1, 0):
-            quantise_part(last, z, z + 1)
-            for j in (2 * z, 2 * z + 1):
-                block_pass(dlts[j][:, 0, :], 1, g, j, 3)
         for z in (1, 0):
             for j in (2 * z, 2 * z + 1):
                 nc.vector.scalar_tensor_tensor(

@@ -22,9 +22,9 @@ NG = NEUR // G
 FLOPS = 2 * ROWS * NEUR * NEUR * 2 + 2 * ROWS * NEUR * D_OUT
 
 V_EVERY = 6
-V_PHASE = 3
+V_PHASE = 1
 LOAD_LEAD = 10
-MULT_LEAD = 3
+MULT_LEAD = 2
 QUANT_LAG = 2
 PI_HI = 3.1415927410125732
 PI_LO = math.pi - PI_HI
@@ -56,7 +56,7 @@ def tile_brainquantumlayer_pc_kernel(
         units = []
         for g in range(NG - 1):
             units.extend((kind, kp, g) for kp in range(4) for kind in range(2))
-        units.extend((kind, kp, NG - 1) for kind in range(2) for kp in range(4))
+        units.extend((kind, kp, NG - 1) for kind in (1, 0) for kp in range(4))
         n_units = len(units)
         raw_m = {}
         raw = {}
@@ -277,7 +277,7 @@ def tile_brainquantumlayer_pc_kernel(
                 code_tiles(u)
                 quantise_part(u, 0, 2)
 
-        def block_pass(ps, kind, g, j, kp):
+        def block_pass(ps, kind, g, j, kp, last_kp=3):
             rc, rs = (st_codes, st_scales) if kind == 0 else (s_codes, s_scales)
             cd, sc = codes[(kind, kp, g)]
             nc.tensor.matmul_mx(
@@ -287,7 +287,7 @@ def tile_brainquantumlayer_pc_kernel(
                 rhs=rc[:, ROWS * kp : ROWS * kp + ROWS].bitcast(FP8X4),
                 rhs_scale=rs[:, ROWS * kp : ROWS * kp + ROWS],
                 start=(kp == 0),
-                stop=(kp == 3),
+                stop=(kp == last_kp),
             )
 
         def big_passes(ps, kind, g, z):
@@ -388,19 +388,26 @@ def tile_brainquantumlayer_pc_kernel(
         last = n_units - 1
         last_tiles = {}
 
-        def last_signal(z):
-            if z == 1:
-                last_tiles["a"] = ep2.tile([P, 4, ROWS], F32, name="a_t", tag="a_t")
-            last_tiles[z] = acc.tile([P, 2, ROWS], F32, name="sig", tag="sig")
-            big_passes(last_tiles[z], 0, NG - 1, z)
+        def last_delta(z):
+            last_tiles[z] = acc.tile([P, 2, ROWS], F32, name="dlt", tag="dlt")
+            big_passes(last_tiles[z], 1, NG - 1, z)
 
-        def last_noise_add(z):
+        def last_delta_times_s(z):
+            if z == 1:
+                last_tiles["c"] = ep1.tile([P, 4, ROWS], F32, name="c_t", tag="c_t")
+            b = 4 * (NG - 1) + 2 * z
+            nc.vector.scalar_tensor_tensor(
+                out=last_tiles["c"][:, 2 * z : 2 * z + 2, :], in0=last_tiles[z][:], scalar=lam_f[:, 0:1],
+                in1=s_t[:, b : b + 2, :], op0=ALU.mult, op1=ALU.mult,
+            )
+
+        def last_add_noise(z):
             for e in range(2):
                 j = 2 * z + e
                 nc.vector.scalar_tensor_tensor(
-                    out=last_tiles["a"][:, j, :], in0=noise_3[:, z, :, e],
+                    out=last_tiles["c"][:, j, :], in0=noise_3[:, z, :, e],
                     scalar=t01[:, 4 * (NG - 1) + j : 4 * (NG - 1) + j + 1],
-                    in1=last_tiles[z][:, e, :], op0=ALU.mult, op1=ALU.add,
+                    in1=last_tiles["c"][:, j, :], op0=ALU.mult, op1=ALU.add,
                 )
 
         plan = {}
@@ -421,7 +428,7 @@ def tile_brainquantumlayer_pc_kernel(
         for q, start in enumerate((14, 17, 22, 26)):
             for gp in range(2):
                 weave(start + 2 * gp, [[pair(wo_transpose, q, gp)], [pair(wo_gather, q, gp)], [pair(wo_quantise, q, gp)]])
-        last_unit = {g: units.index((1, 3, g)) for g in range(NG)}
+        last_unit = {g: units.index((1, 3, g)) for g in range(NG - 1)}
         for g in range(NG - 1):
             pieces = group_pieces(g)
             if g == NG - 2:
@@ -429,7 +436,11 @@ def tile_brainquantumlayer_pc_kernel(
                 pieces = [p[0] + p[1], [], p[3] + p[4], p[5], p[6], [], p[7]]
             weave(last_unit[g] + QUANT_LAG + (3 if g == 0 else 0), pieces)
         weave(last_unit[NG - 2] + 1, [[noise_transpose_last], [noise_last]])
-        weave(n_units - 2, [[pair(last_signal, 1), pair(last_signal, 0)], [pair(last_noise_add, 1), pair(last_noise_add, 0)]])
+        weave(n_units - 3, [
+            [pair(last_delta, 1), pair(last_delta, 0)],
+            [pair(last_delta_times_s, 1), pair(last_delta_times_s, 0), pair(out_add, 0)],
+            [pair(last_add_noise, 1), pair(last_add_noise, 0), pair(out_add, 1)],
+        ])
 
         weave(3, [[bias_spread]])
 
@@ -446,40 +457,33 @@ def tile_brainquantumlayer_pc_kernel(
                 noise_load()
             if u in (5, 9, 13, 17):
                 wo_load((5, 9, 13, 17).index(u))
-            run(plan.get(u, ()))
             multiply_for(u + MULT_LEAD)
+            run(plan.get(u, ()))
 
         for u in sorted(plan):
             if u >= n_units:
                 run(plan[u])
         g = NG - 1
-        a_t = last_tiles["a"]
-        c_t = ep1.tile([P, 4, ROWS], F32, name="c_t", tag="c_t")
-        dlts = {}
+        a_t = ep2.tile([P, 4, ROWS], F32, name="a_t", tag="a_t")
+        sigs = {}
         for j in (2, 3, 0, 1):
-            tag = "dlt" if j >= 2 else "sig"
-            dlts[j] = acc.tile([P, 2, ROWS], F32, name=tag, tag=tag)
+            tag = "sig" if j >= 2 else "dlt"
+            sigs[j] = acc.tile([P, 2, ROWS], F32, name=tag, tag=tag)
             for kp in range(2):
-                block_pass(dlts[j][:, 0, :], 1, g, j, kp)
+                block_pass(sigs[j][:, 0, :], 0, g, j, kp, 2)
         quantise(last)
+        for j in (2, 3, 0, 1):
+            block_pass(sigs[j][:, 0, :], 0, g, j, 3, 2)
         quantise(last - 1)
         for j in (2, 3, 0, 1):
-            for kp in (2, 3):
-                block_pass(dlts[j][:, 0, :], 1, g, j, kp)
-        out_add(0)
-        for z in (1, 0):
-            for j in (2 * z, 2 * z + 1):
-                nc.vector.scalar_tensor_tensor(
-                    out=c_t[:, j, :], in0=dlts[j][:, 0, :], scalar=lam_f[:, 0:1],
-                    in1=s_t[:, 4 * g + j, :], op0=ALU.mult, op1=ALU.mult,
-                )
-        for z in (1, 0):
-            zz = slice(2 * z, 2 * z + 2)
-            nc.vector.tensor_tensor(out=a_t[:, zz, :], in0=a_t[:, zz, :], in1=c_t[:, zz, :], op=ALU.add)
+            block_pass(sigs[j][:, 0, :], 0, g, j, 2, 2)
+        for j in (2, 3, 0, 1):
+            nc.vector.tensor_tensor(
+                out=a_t[:, j, :], in0=sigs[j][:, 0, :], in1=last_tiles["c"][:, j, :], op=ALU.add
+            )
         nsg = ep2.tile([P, ROWS, 4], BF16, name="nsg", tag="nsg", align_bytes=64)
         for mt in range(2):
             tanh_rows(a_t, nsg, P * mt, P * mt + P)
-        out_add(1)
         out_add(2)
         o_sb = natp.tile([P, 4, 512], F32, name="nat", tag="nat")
         for mt in range(2):

@@ -88,11 +88,10 @@ def tile_brainquantumlayer_pc_kernel(
         nc.gpsimd.memset(brow[:], 0.0)
         nc.scalar.dma_start(out=brow[0:1, :], in_=b_out.unsqueeze(0))
         st_nat = natp.tile([P, 2, NEUR], BF16, name="nat", tag="nat")
+        for t in range(2):
+            nc.sync.dma_start(out=st_nat[:, t, :], in_=state[P * t : P * t + P, :])
         for u in range(LOAD_LEAD):
             load_unit(u)
-            if u in (3, 5):
-                t = (3, 5).index(u)
-                nc.sync.dma_start(out=st_nat[:, t, :], in_=state[P * t : P * t + P, :])
         nz_nat = const.tile([P, 2, NEUR], BF16, name="nz_nat")
 
         ident = const.tile([P, P], F32, name="ident")
@@ -244,18 +243,21 @@ def tile_brainquantumlayer_pc_kernel(
                     op=ALU.mult,
                 )
 
-        def regroup_part(gt, u, z0, z1, on_vector):
-            dst = gt[:].rearrange("p (i h r) -> p h i r", i=4, r=8)[:, :, 2 * z0 : 2 * z1, :]
-            srcv = product[u][:].rearrange("p (h d) t i -> p h i (d t)", d=2)[:, :, 2 * z0 : 2 * z1, :]
+        def regroup_part(gt, u, on_vector):
             if on_vector:
-                nc.vector.tensor_copy(out=dst, in_=srcv)
+                nc.vector.tensor_copy(
+                    out=gt[:].rearrange("p (i r) -> p i r", i=4), in_=product[u][:].rearrange("p q t i -> p i (q t)")
+                )
             else:
-                nc.scalar.copy(out=dst, in_=srcv)
+                nc.scalar.copy(
+                    out=gt[:].rearrange("p (i h r) -> p h i r", i=4, r=8),
+                    in_=product[u][:].rearrange("p (h d) t i -> p h i (d t)", d=2),
+                )
 
         def regroup(u):
             gt = grp.tile([P, 2048], BF16, name="grp", tag="grp", align_bytes=64)
             gts[u] = gt
-            regroup_part(gt, u, 0, 2, u % V_EVERY == V_PHASE or u == n_units - 1)
+            regroup_part(gt, u, u % V_EVERY == V_PHASE or u == n_units - 1)
 
         def code_tiles(u):
             kind = units[u][0]
@@ -421,10 +423,7 @@ def tile_brainquantumlayer_pc_kernel(
                 piece()
 
         for gp in range(2):
-            weave(4 + gp, [
-                [pair(state_transpose, gp)], [pair(state_gather, gp)], [pair(state_tanh, gp)],
-                [], [pair(state_round, gp)], [pair(state_quantise, gp)],
-            ])
+            weave(0 + gp, [[], [pair(state_round, gp)], [pair(state_quantise, gp)]])
         for q, start in enumerate((14, 17, 22, 26)):
             for gp in range(2):
                 weave(start + 2 * gp, [[pair(wo_transpose, q, gp)], [pair(wo_gather, q, gp)], [pair(wo_quantise, q, gp)]])
@@ -444,6 +443,10 @@ def tile_brainquantumlayer_pc_kernel(
 
         weave(3, [[bias_spread]])
 
+        for gp in range(2):
+            state_transpose(gp)
+            state_gather(gp)
+            state_tanh(gp)
         for u in range(MULT_LEAD):
             multiply_for(u)
         for u in range(n_units):

@@ -21,7 +21,7 @@ G = 512
 NG = NEUR // G
 FLOPS = 2 * ROWS * NEUR * NEUR * 2 + 2 * ROWS * NEUR * D_OUT
 
-V_EVERY = 6
+V_EVERY = 12
 V_PHASE = 1
 LOAD_LEAD = 10
 MULT_LEAD = 2

from contextlib import ExitStack
import math

import concourse.mybir as mybir
from concourse.masks import make_identity

F32 = mybir.dt.float32
BF16 = mybir.dt.bfloat16
U32 = mybir.dt.uint32
U8 = mybir.dt.uint8
I32 = mybir.dt.int32
FP8X4 = mybir.dt.float8_e4m3fn_x4
ALU = mybir.AluOpType
ACT = mybir.ActivationFunctionType

P = 128
ROWS = 256
NEUR = 2048
D_OUT = 1024
G = 512
NG = NEUR // G
FLOPS = 2 * ROWS * NEUR * NEUR * 2 + 2 * ROWS * NEUR * D_OUT

V_EVERY = 12
V_PHASE = 1
LOAD_LEAD = 10
MULT_LEAD = 2
QUANT_LAG = 2
PI_HI = 3.1415927410125732
PI_LO = math.pi - PI_HI


def tile_brainquantumlayer_pc_kernel(
    tc, state, weights, J, theta, lam, mask, noise_raw, W_out, b_out, out
):
    nc = tc.nc
    with ExitStack() as ctx:
        const = ctx.enter_context(tc.tile_pool(name="const", bufs=1))
        natp = ctx.enter_context(tc.tile_pool(name="natp", bufs=2))
        mpool = ctx.enter_context(tc.tile_pool(name="mpool", bufs=5))
        wpool = ctx.enter_context(tc.tile_pool(name="wpool", bufs=8))
        ppool = ctx.enter_context(tc.tile_pool(name="ppool", bufs=5))
        grp = ctx.enter_context(tc.tile_pool(name="grp", bufs=8))
        cpool = ctx.enter_context(tc.tile_pool(name="cpool", bufs=7))
        ep2 = ctx.enter_context(tc.tile_pool(name="ep2", bufs=2))
        ep1 = ctx.enter_context(tc.tile_pool(name="ep1", bufs=1))
        acc = ctx.enter_context(tc.psum_pool(name="acc", bufs=2))
        trp = ctx.enter_context(tc.psum_pool(name="trp", bufs=4))
        ctx.enter_context(tc.manual_schedule())

        w_v = weights.rearrange("(c p j) n -> c p j n", p=P, j=4)
        j_v = J.rearrange("(c p j) n -> c p j n", p=P, j=4)
        m_v = mask.rearrange("(c p j) n -> c p j n", p=P, j=4)
        wo_v = W_out.rearrange("(q t p) n -> q p t n", t=2, p=P)

        units = []
        for g in range(NG - 1):
            units.extend((kind, kp, g) for kp in range(4) for kind in range(2))
        units.extend((kind, kp, NG - 1) for kind in (1, 0) for kp in range(4))
        n_units = len(units)
        raw_m = {}
        raw = {}

        def load_unit(u):
            if u < n_units:
                kind, kp, g = units[u]
                cols = slice(G * g, G * g + G)
                if (kp, g) not in raw_m:
                    t = mpool.tile([P, 4, G], BF16, name="m_raw", tag="m_raw")
                    nc.sync.dma_start(out=t[:], in_=m_v[kp, :, :, cols])
                    raw_m[(kp, g)] = t
                t = wpool.tile([P, 4, G], BF16, name="raw", tag="raw")
                nc.sync.dma_start(out=t[:], in_=(w_v, j_v)[kind][kp, :, :, cols])
                raw[u] = t

        wo_nat = {}

        def wo_load(q):
            t = natp.tile([P, 2, NEUR], BF16, name="nat", tag="nat")
            nc.sync.dma_start(out=t[:], in_=wo_v[q])
            wo_nat[q] = t

        th = const.tile([P, NG, 4], BF16, name="th")
        nc.scalar.dma_start(out=th[:], in_=theta.rearrange("(g p i) -> p g i", g=NG, i=4))
        lam_bf = const.tile([P, 1], BF16, name="lam_bf")
        nc.scalar.dma_start(out=lam_bf[:], in_=lam.partition_broadcast(P))
        brow = grp.tile([P, D_OUT], BF16, name="grp", tag="grp", align_bytes=64)
        nc.gpsimd.memset(brow[:], 0.0)
        nc.scalar.dma_start(out=brow[0:1, :], in_=b_out.unsqueeze(0))
        st_nat = natp.tile([P, 2, NEUR], BF16, name="nat", tag="nat")
        for t in range(2):
            nc.sync.dma_start(out=st_nat[:, t, :], in_=state[P * t : P * t + P, :])
        for u in range(LOAD_LEAD):
            load_unit(u)
        nz_nat = const.tile([P, 2, NEUR], BF16, name="nz_nat")

        ident = const.tile([P, P], F32, name="ident")
        make_identity(nc, ident[:])
        ones = const.tile([P, P], BF16, name="ones")
        nc.vector.memset(ones[:], 1.0)
        lam_f = const.tile([P, 1], F32, name="lam_f")
        nc.vector.tensor_copy(out=lam_f[:], in_=lam_bf[:])

        th2 = th[:].rearrange("p g i -> p (g i)")
        x2 = const.tile([P, 16], F32, name="x2")
        nc.vector.tensor_scalar(out=x2[:], in0=th2, scalar1=2.0, scalar2=None, op0=ALU.mult)
        ki = const.tile([P, 16], I32, name="ki")
        nc.vector.tensor_scalar(out=ki[:], in0=x2[:], scalar1=1.0 / math.pi, scalar2=None, op0=ALU.mult)
        kf = const.tile([P, 16], F32, name="kf")
        nc.vector.tensor_copy(out=kf[:], in_=ki[:])
        r1 = const.tile([P, 16], F32, name="r1")
        nc.vector.scalar_tensor_tensor(out=r1[:], in0=kf[:], scalar=-PI_HI, in1=x2[:], op0=ALU.mult, op1=ALU.add)
        r2 = const.tile([P, 16], F32, name="r2")
        nc.vector.scalar_tensor_tensor(out=r2[:], in0=kf[:], scalar=-PI_LO, in1=r1[:], op0=ALU.mult, op1=ALU.add)
        sn = const.tile([P, 16], F32, name="sn")
        nc.scalar.activation(out=sn[:], in_=r2[:], func=ACT.Sin)
        t01 = const.tile([P, 16], F32, name="t01")
        nc.scalar.activation(out=t01[:], in_=sn[:], func=ACT.Abs, scale=0.1)

        bias = const.tile([P, D_OUT], BF16, name="bias")

        def bias_spread():
            for oc in range(2):
                pb = trp.tile([P, 512], F32, name="tr", tag="tr")
                nc.tensor.matmul(out=pb[:], lhsT=ones[:], rhs=brow[:, 512 * oc : 512 * oc + 512], start=True, stop=True)
                nc.scalar.copy(out=bias[:, 512 * oc : 512 * oc + 512], in_=pb[:])

        st_codes = const.tile([P, 4 * ROWS], U32, name="st_codes", align_bytes=64)
        st_scales = const.tile([P, 4 * ROWS], U8, name="st_scales", align_bytes=64)
        s_codes = const.tile([P, 4 * ROWS], U32, name="s_codes", align_bytes=64)
        s_scales = const.tile([P, 4 * ROWS], U8, name="s_scales", align_bytes=64)
        s_t = const.tile([P, 16, ROWS], F32, name="s_t")

        def word_view(nat_tile):
            return nat_tile[:].bitcast(F32).rearrange("p t (g c z) -> p t g z c", g=NG, z=2)

        def transposed_bank(words, g):
            bank = trp.tile([P, 2, 256], F32, name="tr", tag="tr")
            for z in range(2):
                for t in range(2):
                    nc.tensor.transpose(bank[:, z, P * t : P * t + P], words[:, t, g, z, :], ident[:])
            return bank

        stgs = {}
        sgs = {}

        state_banks = {}

        def state_transpose(gp):
            for gl in range(2):
                state_banks[2 * gp + gl] = transposed_bank(word_view(st_nat), 2 * gp + gl)

        def state_gather(gp):
            stg = grp.tile([P, 2048], BF16, name="grp", tag="grp", align_bytes=64)
            stg_w = stg[:].bitcast(F32).rearrange("p (g m z) -> p g m z", g=2, z=2)
            for gl in range(2):
                nc.vector.tensor_copy(out=stg_w[:, gl], in_=state_banks[2 * gp + gl][:].rearrange("p z m -> p m z"))
            stgs[gp] = stg

        def state_half(gp):
            return slice(2 * ROWS * gp, 2 * ROWS * (gp + 1))

        def state_tanh(gp):
            nc.scalar.activation(
                out=s_t[:, 8 * gp : 8 * gp + 8, :].rearrange("p (g t) m -> p g t m", g=2),
                in_=stgs[gp][:].rearrange("p (g m t) -> p g t m", g=2, t=4),
                func=ACT.Tanh,
            )
            half = state_half(gp)
            nc.vector.quantize_mx(out=st_codes[:, half].bitcast(FP8X4), scales=st_scales[:, half], in_=stgs[gp][:])

        def state_round(gp):
            sg = grp.tile([P, 2048], BF16, name="grp", tag="grp", align_bytes=64)
            nc.vector.tensor_copy(
                out=sg[:].rearrange("p (g m t) -> p g m t", g=2, t=4),
                in_=s_t[:, 8 * gp : 8 * gp + 8, :].rearrange("p (g t) m -> p g m t", g=2),
            )
            sgs[gp] = sg

        def state_quantise(gp):
            half = state_half(gp)
            nc.vector.quantize_mx(out=s_codes[:, half].bitcast(FP8X4), scales=s_scales[:, half], in_=sgs[gp][:])

        noise_3 = const.tile([P, 2, ROWS, 2], BF16, name="noise_3")

        def noise_load():
            nc.sync.dma_start(out=nz_nat[:], in_=noise_raw.rearrange("(t p) k -> p t k", p=P))

        noise_last_bank = []

        def noise_transpose_last():
            noise_last_bank.append(transposed_bank(word_view(nz_nat), NG - 1))

        def noise_last():
            bank = noise_last_bank[0]
            nc.scalar.copy(out=noise_3[:].rearrange("p z m e -> p (z m e)").bitcast(F32), in_=bank[:].rearrange("p z m -> p (z m)"))

        def noise_bank(g):
            bank = transposed_bank(word_view(nz_nat), g)
            return bank[:].rearrange("p z m -> p (z m)").bitcast(BF16).rearrange("p (z m e) -> p z m e", z=2, e=2)

        wo_codes = const.tile([P, NG, D_OUT], U32, name="wo_codes", align_bytes=64)
        wo_scales = const.tile([P, NG, D_OUT], U8, name="wo_scales", align_bytes=64)
        wo_gt = {}

        wo_banks = {}

        def wo_transpose(q, gp):
            for gl in range(2):
                wo_banks[(q, 2 * gp + gl)] = transposed_bank(word_view(wo_nat[q]), 2 * gp + gl)

        def wo_gather(q, gp):
            gt = grp.tile([P, 2048], BF16, name="grp", tag="grp", align_bytes=64)
            gw = gt[:].bitcast(F32).rearrange("p (g o z) -> p g o z", g=2, z=2)
            for gl in range(2):
                nc.scalar.copy(out=gw[:, gl], in_=wo_banks[(q, 2 * gp + gl)][:].rearrange("p z o -> p o z"))
            wo_gt[(q, gp)] = gt

        def wo_quantise(q, gp):
            cols = slice(256 * q, 256 * q + 256)
            for gl in range(2):
                nc.vector.quantize_mx(
                    out=wo_codes[:, 2 * gp + gl, cols].bitcast(FP8X4),
                    scales=wo_scales[:, 2 * gp + gl, cols],
                    in_=wo_gt[(q, gp)][:, 1024 * gl : 1024 * gl + 1024],
                )

        ns_codes = const.tile([P, NG * ROWS], U32, name="ns_codes", align_bytes=64)
        ns_scales = const.tile([P, NG * ROWS], U8, name="ns_scales", align_bytes=64)
        codes = {}
        gts = {}

        product = {}

        def multiply_for(u):
            if u < n_units:
                kind, kp, g = units[u]
                product[u] = ppool.tile([P, P, 4, 4], BF16, name="product", tag="product")
                nc.vector.tensor_tensor(
                    out=product[u][:],
                    in0=raw[u][:].rearrange("p t (q i) -> p q t i", i=4),
                    in1=raw_m[(kp, g)][:].rearrange("p t (q i) -> p q t i", i=4),
                    op=ALU.mult,
                )

        def regroup_part(gt, u, on_vector):
            if on_vector:
                nc.vector.tensor_copy(
                    out=gt[:].rearrange("p (i r) -> p i r", i=4), in_=product[u][:].rearrange("p q t i -> p i (q t)")
                )
            else:
                nc.scalar.copy(
                    out=gt[:].rearrange("p (i h r) -> p h i r", i=4, r=8),
                    in_=product[u][:].rearrange("p (h d) t i -> p h i (d t)", d=2),
                )

        def regroup(u):
            gt = grp.tile([P, 2048], BF16, name="grp", tag="grp", align_bytes=64)
            gts[u] = gt
            regroup_part(gt, u, u % V_EVERY == V_PHASE or u == n_units - 1)

        def code_tiles(u):
            kind = units[u][0]
            tagc = "cw" if kind == 0 else "cj"
            tags = "sw" if kind == 0 else "sj"
            cd = cpool.tile([P, G], U32, name=tagc, tag=tagc, align_bytes=64)
            sc = cpool.tile([P, G], U8, name=tags, tag=tags, align_bytes=64)
            codes[units[u]] = (cd, sc)

        def quantise_part(u, z0, z1):
            cd, sc = codes[units[u]]
            cols = slice(256 * z0, 256 * z1)
            nc.vector.quantize_mx(
                out=cd[:, cols].bitcast(FP8X4), scales=sc[:, cols], in_=gts[u][:, 1024 * z0 : 1024 * z1]
            )

        def quantise(u):
            if 0 <= u < n_units:
                code_tiles(u)
                quantise_part(u, 0, 2)

        def block_pass(ps, kind, g, j, kp, last_kp=3):
            rc, rs = (st_codes, st_scales) if kind == 0 else (s_codes, s_scales)
            cd, sc = codes[(kind, kp, g)]
            nc.tensor.matmul_mx(
                out=ps,
                lhsT=cd[:, P * j : P * j + P].bitcast(FP8X4),
                lhsT_scale=sc[:, P * j : P * j + P],
                rhs=rc[:, ROWS * kp : ROWS * kp + ROWS].bitcast(FP8X4),
                rhs_scale=rs[:, ROWS * kp : ROWS * kp + ROWS],
                start=(kp == 0),
                stop=(kp == last_kp),
            )

        def big_passes(ps, kind, g, z):
            for e in range(2):
                for kp in range(4):
                    block_pass(ps[:, e, :], kind, g, 2 * z + e, kp)

        def tanh_rows(a_t, nsg, m0, m1):
            nc.scalar.activation(out=nsg[:, m0:m1, :], in_=a_t[:, :, m0:m1].rearrange("p t m -> p m t"), func=ACT.Tanh)

        def quantise_rows(nsg, g, m0, m1):
            nc.vector.quantize_mx(
                out=ns_codes[:, ROWS * g + m0 : ROWS * g + m1].bitcast(FP8X4),
                scales=ns_scales[:, ROWS * g + m0 : ROWS * g + m1],
                in_=nsg[:, m0:m1, :].rearrange("p m t -> p (m t)"),
            )

        def pair(fn, *args):
            return lambda: fn(*args)

        def group_pieces(g):
            tiles = {}

            def products(z):
                sig = acc.tile([P, 2, ROWS], F32, name="sig", tag="sig")
                dlt = acc.tile([P, 2, ROWS], F32, name="dlt", tag="dlt")
                tiles[("sig", z)] = sig
                tiles[("dlt", z)] = dlt
                big_passes(sig, 0, g, z)
                big_passes(dlt, 1, g, z)

            def delta_times_s(z):
                if z == 0:
                    tiles["c"] = ep1.tile([P, 4, ROWS], F32, name="c_t", tag="c_t")
                nc.vector.scalar_tensor_tensor(
                    out=tiles["c"][:, 2 * z : 2 * z + 2, :], in0=tiles[("dlt", z)][:], scalar=lam_f[:, 0:1],
                    in1=s_t[:, 4 * g + 2 * z : 4 * g + 2 * z + 2, :], op0=ALU.mult, op1=ALU.mult,
                )

            def add_noise(z):
                for j in (2 * z, 2 * z + 1):
                    nc.vector.scalar_tensor_tensor(
                        out=tiles["c"][:, j, :], in0=tiles["noise"][:, z, :, j % 2],
                        scalar=t01[:, 4 * g + j : 4 * g + j + 1],
                        in1=tiles["c"][:, j, :], op0=ALU.mult, op1=ALU.add,
                    )

            def add_signal(z):
                if z == 0:
                    tiles["a"] = ep2.tile([P, 4, ROWS], F32, name="a_t", tag="a_t")
                nc.vector.tensor_tensor(
                    out=tiles["a"][:, 2 * z : 2 * z + 2, :], in0=tiles[("sig", z)][:],
                    in1=tiles["c"][:, 2 * z : 2 * z + 2, :], op=ALU.add,
                )

            def transpose_noise():
                tiles["noise"] = noise_bank(g)

            def tanh():
                tiles["ns"] = ep2.tile([P, ROWS, 4], BF16, name="nsg", tag="nsg", align_bytes=64)
                tanh_rows(tiles["a"], tiles["ns"], 0, ROWS)

            def last():
                quantise_rows(tiles["ns"], g, 0, ROWS)

            return [
                [pair(products, 0)],
                [pair(products, 1), transpose_noise],
                [],
                [pair(delta_times_s, 0)],
                [pair(delta_times_s, 1), pair(add_noise, 0)],
                [pair(add_noise, 1), pair(add_signal, 0)],
                [pair(add_signal, 1), tanh],
                [last],
            ]

        ob = {}

        def out_pass(g, mt, oc):
            lo = ROWS * g + P * mt
            nc.tensor.matmul_mx(
                out=ob[(mt, oc)][:],
                lhsT=ns_codes[:, lo : lo + P].bitcast(FP8X4),
                lhsT_scale=ns_scales[:, lo : lo + P],
                rhs=wo_codes[:, g, 512 * oc : 512 * oc + 512].bitcast(FP8X4),
                rhs_scale=wo_scales[:, g, 512 * oc : 512 * oc + 512],
                start=(g == 0),
                stop=(g == NG - 1),
            )

        def out_add(g):
            for mt in range(2):
                for oc in range(2):
                    if g == 0:
                        ob[(mt, oc)] = trp.tile([P, 512], F32, name="tr", tag="tr")
                    out_pass(g, mt, oc)

        last = n_units - 1
        last_tiles = {}

        def last_delta(z):
            last_tiles[z] = acc.tile([P, 2, ROWS], F32, name="dlt", tag="dlt")
            big_passes(last_tiles[z], 1, NG - 1, z)

        def last_delta_times_s(z):
            if z == 1:
                last_tiles["c"] = ep1.tile([P, 4, ROWS], F32, name="c_t", tag="c_t")
            b = 4 * (NG - 1) + 2 * z
            nc.vector.scalar_tensor_tensor(
                out=last_tiles["c"][:, 2 * z : 2 * z + 2, :], in0=last_tiles[z][:], scalar=lam_f[:, 0:1],
                in1=s_t[:, b : b + 2, :], op0=ALU.mult, op1=ALU.mult,
            )

        def last_add_noise(z):
            for e in range(2):
                j = 2 * z + e
                nc.vector.scalar_tensor_tensor(
                    out=last_tiles["c"][:, j, :], in0=noise_3[:, z, :, e],
                    scalar=t01[:, 4 * (NG - 1) + j : 4 * (NG - 1) + j + 1],
                    in1=last_tiles["c"][:, j, :], op0=ALU.mult, op1=ALU.add,
                )

        plan = {}

        def weave(start, pieces):
            for i, group in enumerate(pieces):
                plan.setdefault(start + i, []).extend(group)

        def run(pieces):
            for piece in pieces:
                piece()

        for gp in range(2):
            weave(0 + gp, [[], [pair(state_round, gp)], [pair(state_quantise, gp)]])
        for q, start in enumerate((14, 17, 22, 26)):
            for gp in range(2):
                weave(start + 2 * gp, [[pair(wo_transpose, q, gp)], [pair(wo_gather, q, gp)], [pair(wo_quantise, q, gp)]])
        last_unit = {g: units.index((1, 3, g)) for g in range(NG - 1)}
        for g in range(NG - 1):
            pieces = group_pieces(g)
            if g == NG - 2:
                p = pieces
                pieces = [p[0] + p[1], [], p[3] + p[4], p[5], p[6], [], p[7]]
            weave(last_unit[g] + QUANT_LAG + (3 if g == 0 else 0), pieces)
        weave(last_unit[NG - 2] + 1, [[noise_transpose_last], [noise_last]])
        weave(n_units - 3, [
            [pair(last_delta, 1), pair(last_delta, 0)],
            [pair(last_delta_times_s, 1), pair(last_delta_times_s, 0), pair(out_add, 0)],
            [pair(last_add_noise, 1), pair(last_add_noise, 0), pair(out_add, 1)],
        ])

        weave(3, [[bias_spread]])

        for gp in range(2):
            state_transpose(gp)
            state_gather(gp)
            state_tanh(gp)
        for u in range(MULT_LEAD):
            multiply_for(u)
        for u in range(n_units):
            if u < n_units - 1:
                regroup(u)
            quantise(u - QUANT_LAG)
            if u == n_units - 2:
                regroup(n_units - 1)
            load_unit(u + LOAD_LEAD)
            if u == 3:
                noise_load()
            if u in (5, 9, 13, 17):
                wo_load((5, 9, 13, 17).index(u))
            multiply_for(u + MULT_LEAD)
            run(plan.get(u, ()))

        for u in sorted(plan):
            if u >= n_units:
                run(plan[u])
        g = NG - 1
        a_t = ep2.tile([P, 4, ROWS], F32, name="a_t", tag="a_t")
        sigs = {}
        for j in (2, 3, 0, 1):
            tag = "sig" if j >= 2 else "dlt"
            sigs[j] = acc.tile([P, 2, ROWS], F32, name=tag, tag=tag)
            for kp in range(2):
                block_pass(sigs[j][:, 0, :], 0, g, j, kp, 2)
        quantise(last)
        for j in (2, 3, 0, 1):
            block_pass(sigs[j][:, 0, :], 0, g, j, 3, 2)
        quantise(last - 1)
        for j in (2, 3, 0, 1):
            block_pass(sigs[j][:, 0, :], 0, g, j, 2, 2)
        for j in (2, 3, 0, 1):
            nc.vector.tensor_tensor(
                out=a_t[:, j, :], in0=sigs[j][:, 0, :], in1=last_tiles["c"][:, j, :], op=ALU.add
            )
        nsg = ep2.tile([P, ROWS, 4], BF16, name="nsg", tag="nsg", align_bytes=64)
        for mt in range(2):
            tanh_rows(a_t, nsg, P * mt, P * mt + P)
        out_add(2)
        o_sb = natp.tile([P, 4, 512], F32, name="nat", tag="nat")
        for mt in range(2):
            quantise_rows(nsg, g, P * mt, P * mt + P)
            for oc in range(2):
                out_pass(g, mt, oc)
        for mt in range(2):
            for oc in range(2):
                cols = slice(512 * oc, 512 * oc + 512)
                o_part = o_sb[:, 2 * mt + oc, :]
                nc.vector.tensor_tensor(out=o_part, in0=ob[(mt, oc)][:], in1=bias[:, cols], op=ALU.add)
                nc.sync.dma_start(out=out[P * mt : P * mt + P, cols], in_=o_part)
